import numpy as np
import ml_dtypes


def mxq(x, axis, fmt="e4m3"):
    dtype, down = {"e4m3": (ml_dtypes.float8_e4m3fn, 7), "e5m2": (ml_dtypes.float8_e5m2, 14)}[fmt]
    v = np.moveaxis(np.asarray(x, np.float32).astype(ml_dtypes.bfloat16).astype(np.float64), axis, -1)
    blocks = v.reshape(v.shape[:-1] + (-1, 32))
    amax = np.abs(blocks).max(-1, keepdims=True)
    byte = np.maximum(np.where(amax > 0, np.frexp(amax)[1] - 1 + 127, 0) - down, 1)
    scale = np.exp2(byte - 127.0)
    codes = (blocks / scale).astype(np.float32).astype(dtype).astype(np.float64)
    return np.moveaxis((codes * scale).reshape(v.shape), -1, axis)


WIDE = False


def mx_kscale(k):
    if not WIDE:
        return np.ones(k)
    levels = np.array([10, -10, 5, -5, 0])
    a = np.random.permutation(np.resize(levels, k // 512 * 4)).reshape(k // 512, 4)
    idx = np.arange(k)
    return np.exp2(a[idx // 512, idx % 128 // 32])


BF16 = ml_dtypes.bfloat16


def bf(x):
    return np.asarray(x, np.float32).astype(BF16)


def f64(x):
    return np.asarray(x).astype(np.float64)


E2M1 = np.array([0.0, 0.5, 1.0, 1.5, 2.0, 3.0, 4.0, 6.0, -0.0, -0.5, -1.0, -1.5, -2.0, -3.0, -4.0, -6.0])


def pack_weight(w, fmt):
    k, n = w.shape
    w = f64(bf(w)).reshape(k // 32, 32, n)
    amax = np.abs(w).max(1)
    if fmt == "e4m3":
        byte = np.frexp(amax)[1] - 1 + 127 - 7
    else:
        mant, ex = np.frexp(amax / 6.0)
        byte = np.where(mant > 0.5, ex, ex - 1) + 127
    byte = np.clip(np.where(amax > 0, byte, 1), 1, 254)
    scaled = (w * np.exp2(127.0 - byte)[:, None, :]).reshape(k, n).astype(np.float32)
    by_word = np.ascontiguousarray(scaled.reshape(k // 512, 128, 4, n).transpose(0, 1, 3, 2))
    if fmt == "e4m3":
        words = by_word.astype(ml_dtypes.float8_e4m3fn).view(np.uint8)
    else:
        c = by_word.astype(ml_dtypes.float4_e2m1fn).view(np.uint8) & 0xF
        words = c[..., 0::2] | (c[..., 1::2] << 4)
    return np.ascontiguousarray(words), np.ascontiguousarray(byte.astype(np.uint8).reshape(k // 512, 16, n))


def unpack_weight(words, scales, fmt):
    g, p, n, _ = words.shape
    if fmt == "e4m3":
        vals = np.ascontiguousarray(words).view(ml_dtypes.float8_e4m3fn).astype(np.float64)
    else:
        nib = np.empty((g, p, n, 4), np.uint8)
        nib[..., 0::2] = words & 0xF
        nib[..., 1::2] = words >> 4
        vals = E2M1[nib]
    vals = vals * np.repeat(np.exp2(scales.astype(np.float64) - 127.0), 8, axis=1)[..., None]
    return vals.transpose(0, 1, 3, 2).reshape(g * 512, n)


B, CIN, H, W, CP, G = 3, 2048, 16, 16, 1024, 2
CG = CP // G
CO = CIN // G
HW = H * W
EPS = 1e-5


def setup_inputs():
    s = mx_kscale(CG)
    y = bf((np.random.standard_normal((B, G, CG, HW)) * 2.5 + 1.0) * s[None, None, :, None])
    stack = ((np.random.standard_normal((G, CO, CG)) / np.sqrt(CG) + 1.5 / CG) / s).swapaxes(1, 2)
    words, scales = pack_weight(stack.reshape(-1, CO), "e4m3")
    return {"y": y,
            "Wz_words": words,
            "Wz_scales": scales,
            "gamma": bf(1.0 + 0.1 * np.random.standard_normal(CIN)),
            "beta": bf(0.1 * np.random.standard_normal(CIN)),
            "x": bf(np.random.standard_normal((B, CIN, H, W)))}


def reference(y, Wz_words, Wz_scales, gamma, beta, x):
    wq = unpack_weight(Wz_words, Wz_scales, "e4m3").reshape(G, CG, CO).swapaxes(1, 2)
    z = wq @ mxq(f64(y), 2, "e4m3")
    zr = z.reshape(B, G, CO * HW)
    mu = zr.mean(-1, keepdims=True)
    var = zr.var(-1, keepdims=True)
    zn = ((zr - mu) * (1.0 / np.sqrt(var + EPS))).reshape(B, CIN, H, W)
    return zn * f64(gamma)[None, :, None, None] + f64(beta)[None, :, None, None] + f64(x)

@@ -1,0 +1,267 @@
+from contextlib import ExitStack
+
+import concourse.mybir as mybir
+from concourse.masks import make_identity
+
+F32 = mybir.dt.float32
+BF16 = mybir.dt.bfloat16
+I32 = mybir.dt.int32
+U32 = mybir.dt.uint32
+U8 = mybir.dt.uint8
+FP8X4 = mybir.dt.float8_e4m3fn_x4
+ALU = mybir.AluOpType
+ACT = mybir.ActivationFunctionType
+
+IMAGES = 3
+GROUPS = 2
+K = 512
+CHANNELS = 1024
+POSITIONS = 256
+EPS = 1e-5
+
+P = 128
+PACK = 4
+TILES = CHANNELS // P
+TILES_PER_BANK = 512 // POSITIONS
+BANK_COLS = TILES_PER_BANK * POSITIONS
+BANKS = TILES // TILES_PER_BANK
+SCALAR_BANKS = 2
+VECTOR_BANKS = BANKS - SCALAR_BANKS
+PIECE_TILES = 4
+PIECES = TILES // PIECE_TILES
+QUADRANTS = 4
+BLOCKS_PER_QUADRANT = 4
+BN_STATS_DIM = 6
+COUNT = CHANNELS * POSITIONS
+AHEAD = 2
+
+FLOPS = 2 * IMAGES * GROUPS * CHANNELS * K * POSITIONS
+
+
+def tile_spatialcgnl_pb_e_kernel(tc, y, Wz_words, Wz_scales, gamma, beta, x, out):
+    nc = tc.nc
+    slabs = [(j, b) for j in range(GROUPS) for b in range(IMAGES)]
+
+    y_rows = y.rearrange("b j (p t) n -> b j p t n", t=PACK)
+    x_rows = x.rearrange("b (r p) h w -> b p r (h w)", p=P)
+    out_rows = out.rearrange("b (r p) h w -> b p r (h w)", p=P)
+    words_i32 = Wz_words.rearrange("j p n t -> j p (n t)").bitcast(I32)
+    scales_i32 = Wz_scales.bitcast(I32)
+    gamma_rows = gamma.rearrange("(r p) -> r p", p=P)
+    beta_rows = beta.rearrange("(r p) -> r p", p=P)
+    affine_rows = GROUPS * TILES
+
+    with ExitStack() as ctx:
+        ctx.enter_context(tc.manual_schedule())
+        keep = ctx.enter_context(tc.tile_pool(name="keep", bufs=1))
+        small = ctx.enter_context(tc.tile_pool(name="small", bufs=3))
+        scratch = ctx.enter_context(tc.tile_pool(name="scratch", bufs=4))
+        psum_scalar = ctx.enter_context(tc.psum_pool(name="psum_scalar", bufs=SCALAR_BANKS + 1))
+        psum_vector = ctx.enter_context(tc.psum_pool(name="psum_vector", bufs=2 * VECTOR_BANKS))
+        psum_small = ctx.enter_context(tc.psum_pool(name="psum_small", bufs=1))
+
+        w_words = keep.tile([P, GROUPS, CHANNELS], U32, align_bytes=64)
+        w_planes = keep.tile([P, CHANNELS], U8, align_bytes=64)
+        y_raw = keep.tile([P, len(slabs), PACK, POSITIONS], BF16)
+        y_grouped = keep.tile([P, len(slabs), POSITIONS, PACK], BF16, align_bytes=64)
+        y_words = keep.tile([P, len(slabs), POSITIONS], U32, align_bytes=64)
+        y_planes = keep.tile([P, len(slabs), POSITIONS], U8, align_bytes=64)
+        x_sb = keep.tile([P, len(slabs), TILES, POSITIONS], BF16)
+        result = keep.tile([P, len(slabs), TILES, POSITIONS], F32)
+
+        nc.vector.memset(w_planes[:].bitcast(I32), 0)
+        affine_in = keep.tile([P, P], BF16)
+        nc.vector.memset(affine_in[:], 0.0)
+        nc.scalar.dma_start(out=affine_in[0:affine_rows, :], in_=gamma_rows)
+        nc.scalar.dma_start(out=affine_in[affine_rows : 2 * affine_rows, :], in_=beta_rows)
+        eps = keep.tile([P, 1], F32)
+        nc.vector.memset(eps[:], EPS)
+        warm = keep.tile([P, 1], F32)
+        nc.scalar.activation(out=warm[:], in_=eps[:], func=ACT.Sqrt)
+        share_vector = keep.tile([P, P], F32)
+        nc.vector.memset(share_vector[:], -float(VECTOR_BANKS * BANK_COLS) / COUNT)
+        share_scalar = keep.tile([P, P], F32)
+        nc.vector.memset(share_scalar[:], -1.0 / COUNT)
+        identity = keep.tile([P, P], BF16)
+        make_identity(nc, identity[:])
+
+        def load_weight(j):
+            for half in range(2):
+                cols = slice(half * CHANNELS // 2, (half + 1) * CHANNELS // 2)
+                nc.sync.dma_start(out=w_words[:, j, cols].bitcast(I32), in_=words_i32[j, :, cols])
+
+        def load_y(u):
+            j, b = slabs[u]
+            nc.sync.dma_start(out=y_raw[:, u], in_=y_rows[b, j])
+
+        def load_x(u):
+            j, b = slabs[u]
+            for piece in range(PIECES):
+                first = piece * PIECE_TILES
+                tiles = slice(first, first + PIECE_TILES)
+                rows = slice(j * TILES + first, j * TILES + first + PIECE_TILES)
+                nc.sync.dma_start(out=x_sb[:, u, tiles, :], in_=x_rows[b, :, rows, :])
+
+        live = GROUPS * BLOCKS_PER_QUADRANT
+        for quadrant in range(QUADRANTS):
+            blocks = slice(quadrant * BLOCKS_PER_QUADRANT, (quadrant + 1) * BLOCKS_PER_QUADRANT)
+            nc.sync.dma_start(
+                out=w_planes[:].bitcast(I32)[32 * quadrant : 32 * quadrant + live, :],
+                in_=scales_i32[:, blocks, :],
+            )
+        for j in range(GROUPS):
+            head = j * IMAGES
+            load_y(head)
+            load_weight(j)
+            for u in range(head + 1, head + IMAGES):
+                load_y(u)
+            for u in range(head, head + IMAGES):
+                load_x(u)
+
+        affine_cols = keep.tile([P, 2 * affine_rows], F32)
+
+        def spread_affine():
+            affine_ps = psum_small.tile([P, P], BF16, tag="small")
+            nc.tensor.transpose(affine_ps[:], affine_in[:], identity[:])
+            nc.vector.tensor_copy(out=affine_cols[:], in_=affine_ps[:, 0 : 2 * affine_rows])
+
+        banks_of = {}
+        neg_mean_of = {}
+        var_of = {}
+        gain_of = {}
+        shift_of = {}
+
+        def quantise(u):
+            nc.vector.tensor_copy(
+                out=y_grouped[:, u].rearrange("p (c i) t -> p c t i", i=4),
+                in_=y_raw[:, u].rearrange("p t (c i) -> p c t i", i=4),
+            )
+            nc.vector.quantize_mx(
+                out=y_words[:, u, :].bitcast(FP8X4),
+                scales=y_planes[:, u, :],
+                in_=y_grouped[:, u].rearrange("p n t -> p (n t)"),
+            )
+
+        def multiply(u):
+            j = slabs[u][0]
+            banks = []
+            for k in range(BANKS):
+                home = psum_scalar if k < SCALAR_BANKS else psum_vector
+                bank = home.tile([P, TILES_PER_BANK, POSITIONS], F32)
+                for t in range(TILES_PER_BANK):
+                    m = k * TILES_PER_BANK + t
+                    cols = slice(m * P, (m + 1) * P)
+                    nc.tensor.matmul_mx(
+                        out=bank[:, t, :],
+                        lhsT=w_words[:, j, cols].bitcast(FP8X4),
+                        lhsT_scale=w_planes[BLOCKS_PER_QUADRANT * j : P, cols],
+                        rhs=y_words[:, u, :].bitcast(FP8X4),
+                        rhs_scale=y_planes[:, u, :],
+                        start=True,
+                        stop=True,
+                    )
+                banks.append(bank)
+            banks_of[u] = banks
+
+        def statistics(u):
+            j = slabs[u][0]
+            banks = banks_of[u]
+            sums = small.tile([P, SCALAR_BANKS, 2], F32)
+            for k in range(SCALAR_BANKS):
+                z = banks[k][:].rearrange("p t n -> p (t n)")
+                tiles = slice(k * TILES_PER_BANK, (k + 1) * TILES_PER_BANK)
+                nc.scalar.activation(
+                    out=result[:, u, tiles, :].rearrange("p t n -> p (t n)"),
+                    in_=z,
+                    func=ACT.Identity,
+                    accum_out=sums[:, k, 0:1],
+                )
+                squares = scratch.tile([P, BANK_COLS], BF16)
+                nc.scalar.activation(out=squares[:], in_=z, func=ACT.Square, accum_out=sums[:, k, 1:2])
+            moments = small.tile([P, VECTOR_BANKS, BN_STATS_DIM], F32)
+            for k in range(VECTOR_BANKS):
+                z = banks[SCALAR_BANKS + k][:].rearrange("p t n -> p (t n)")
+                nc.vector.bn_stats(out=moments[:, k, :], in_=z)
+            means = small.tile([P, 2], F32)
+            nc.vector.bn_aggr(out=means[:], in_=moments[:].rearrange("p k s -> p (k s)"))
+            nc.vector.scalar_tensor_tensor(
+                out=means[:, 1:2],
+                in0=means[:, 0:1],
+                scalar=means[:, 0:1],
+                in1=means[:, 1:2],
+                op0=ALU.mult,
+                op1=ALU.add,
+            )
+            totals = psum_small.tile([P, 2], F32, tag="small")
+            nc.tensor.matmul(out=totals[:], lhsT=share_vector[:], rhs=means[:], start=True, stop=False)
+            for k in range(SCALAR_BANKS):
+                nc.tensor.matmul(
+                    out=totals[:],
+                    lhsT=share_scalar[:],
+                    rhs=sums[:, k, :],
+                    start=False,
+                    stop=(k == SCALAR_BANKS - 1),
+                )
+            neg_mean = totals[:, 0:1]
+            neg_square = totals[:, 1:2]
+            neg_var = small.tile([P, 1], F32)
+            nc.vector.tensor_scalar(
+                out=neg_var[:], in0=neg_mean, scalar1=neg_mean, scalar2=neg_square, op0=ALU.mult, op1=ALU.add
+            )
+            var = small.tile([P, 1], F32)
+            nc.vector.tensor_scalar(
+                out=var[:], in0=neg_var[:], scalar1=-1.0, scalar2=0.0, op0=ALU.mult, op1=ALU.max
+            )
+            neg_mean_of[u] = neg_mean
+            var_of[u] = var
+
+        def coefficients(u):
+            j = slabs[u][0]
+            std = small.tile([P, 1], F32)
+            nc.scalar.activation(out=std[:], in_=var_of[u][:], func=ACT.Sqrt, bias=eps[:])
+            rstd = small.tile([P, 1], F32)
+            nc.vector.reciprocal(out=rstd[:], in_=std[:])
+            gamma_cols = affine_cols[:, j * TILES : (j + 1) * TILES]
+            beta_cols = affine_cols[:, affine_rows + j * TILES : affine_rows + (j + 1) * TILES]
+            gain = small.tile([P, TILES], F32)
+            nc.vector.tensor_scalar_mul(out=gain[:], in0=gamma_cols, scalar1=rstd[:])
+            shift = small.tile([P, TILES], F32)
+            nc.vector.scalar_tensor_tensor(
+                out=shift[:], in0=gain[:], scalar=neg_mean_of[u], in1=beta_cols, op0=ALU.mult, op1=ALU.add
+            )
+            gain_of[u] = gain
+            shift_of[u] = shift
+
+        def finish(u):
+            j, b = slabs[u]
+            for piece in reversed(range(PIECES)):
+                first = piece * PIECE_TILES
+                tiles = slice(first, first + PIECE_TILES)
+                for m in range(first, first + PIECE_TILES):
+                    k, t = divmod(m, TILES_PER_BANK)
+                    z = result[:, u, m, :] if k < SCALAR_BANKS else banks_of[u][k][:, t, :]
+                    nc.scalar.activation(
+                        out=result[:, u, m, :],
+                        in_=z,
+                        func=ACT.Identity,
+                        scale=gain_of[u][:, m : m + 1],
+                        bias=shift_of[u][:, m : m + 1],
+                    )
+                nc.vector.tensor_tensor(
+                    out=result[:, u, tiles, :], in0=result[:, u, tiles, :], in1=x_sb[:, u, tiles, :], op=ALU.add
+                )
+                rows = slice(j * TILES + first, j * TILES + first + PIECE_TILES)
+                nc.sync.dma_start(out=out_rows[b, :, rows, :], in_=result[:, u, tiles, :])
+
+        quantise(0)
+        spread_affine()
+        quantise(1)
+        for u in range(len(slabs)):
+            multiply(u)
+            statistics(u)
+            if u > 0:
+                finish(u - 1)
+            coefficients(u)
+            if u + AHEAD < len(slabs):
+                quantise(u + AHEAD)
+        finish(len(slabs) - 1)

@@ -24,11 +24,9 @@ PACK = 4
 TILES = CHANNELS // P
 TILES_PER_BANK = 512 // POSITIONS
 BANK_COLS = TILES_PER_BANK * POSITIONS
-BANKS = TILES // TILES_PER_BANK
-SCALAR_BANKS = 2
-VECTOR_BANKS = BANKS - SCALAR_BANKS
-PIECE_TILES = 4
-PIECES = TILES // PIECE_TILES
+PIECES = 2
+PIECE_TILES = TILES // PIECES
+PIECE_BANKS = PIECE_TILES // TILES_PER_BANK
 QUADRANTS = 4
 BLOCKS_PER_QUADRANT = 4
 BN_STATS_DIM = 6
@@ -41,6 +39,7 @@ FLOPS = 2 * IMAGES * GROUPS * CHANNELS * K * POSITIONS
 def tile_spatialcgnl_pb_e_kernel(tc, y, Wz_words, Wz_scales, gamma, beta, x, out):
     nc = tc.nc
     slabs = [(j, b) for j in range(GROUPS) for b in range(IMAGES)]
+    n_slabs = len(slabs)
 
     y_rows = y.rearrange("b j (p t) n -> b j p t n", t=PACK)
     x_rows = x.rearrange("b (r p) h w -> b p r (h w)", p=P)
@@ -56,18 +55,18 @@ def tile_spatialcgnl_pb_e_kernel(tc, y, Wz_words, Wz_scales, gamma, beta, x, out
         keep = ctx.enter_context(tc.tile_pool(name="keep", bufs=1))
         small = ctx.enter_context(tc.tile_pool(name="small", bufs=3))
         scratch = ctx.enter_context(tc.tile_pool(name="scratch", bufs=4))
-        psum_scalar = ctx.enter_context(tc.psum_pool(name="psum_scalar", bufs=SCALAR_BANKS + 1))
-        psum_vector = ctx.enter_context(tc.psum_pool(name="psum_vector", bufs=2 * VECTOR_BANKS))
+        psum_piece0 = ctx.enter_context(tc.psum_pool(name="psum_piece0", bufs=PIECE_BANKS + 1))
+        psum_piece1 = ctx.enter_context(tc.psum_pool(name="psum_piece1", bufs=2 * PIECE_BANKS))
         psum_small = ctx.enter_context(tc.psum_pool(name="psum_small", bufs=1))
 
         w_words = keep.tile([P, GROUPS, CHANNELS], U32, align_bytes=64)
         w_planes = keep.tile([P, CHANNELS], U8, align_bytes=64)
-        y_raw = keep.tile([P, len(slabs), PACK, POSITIONS], BF16)
-        y_grouped = keep.tile([P, len(slabs), POSITIONS, PACK], BF16, align_bytes=64)
-        y_words = keep.tile([P, len(slabs), POSITIONS], U32, align_bytes=64)
-        y_planes = keep.tile([P, len(slabs), POSITIONS], U8, align_bytes=64)
-        x_sb = keep.tile([P, len(slabs), TILES, POSITIONS], BF16)
-        result = keep.tile([P, len(slabs), TILES, POSITIONS], F32)
+        y_raw = keep.tile([P, n_slabs, PACK, POSITIONS], BF16)
+        y_grouped = keep.tile([P, n_slabs, POSITIONS, PACK], BF16, align_bytes=64)
+        y_words = keep.tile([P, n_slabs, POSITIONS], U32, align_bytes=64)
+        y_planes = keep.tile([P, n_slabs, POSITIONS], U8, align_bytes=64)
+        x_sb = keep.tile([P, n_slabs, PIECES, PIECE_TILES, POSITIONS], BF16)
+        result = keep.tile([P, n_slabs, PIECES, PIECE_TILES, POSITIONS], F32)
 
         nc.vector.memset(w_planes[:].bitcast(I32), 0)
         affine_in = keep.tile([P, P], BF16)
@@ -77,17 +76,17 @@ def tile_spatialcgnl_pb_e_kernel(tc, y, Wz_words, Wz_scales, gamma, beta, x, out
         eps = keep.tile([P, 1], F32)
         nc.vector.memset(eps[:], EPS)
         warm = keep.tile([P, 1], F32)
-        nc.scalar.activation(out=warm[:], in_=eps[:], func=ACT.Sqrt)
-        share_vector = keep.tile([P, P], F32)
-        nc.vector.memset(share_vector[:], -float(VECTOR_BANKS * BANK_COLS) / COUNT)
-        share_scalar = keep.tile([P, P], F32)
-        nc.vector.memset(share_scalar[:], -1.0 / COUNT)
+        nc.scalar.activation(out=warm[:], in_=eps[:], func=ACT.Abs_reciprocal_sqrt)
+        share_of_means = keep.tile([P, P], F32)
+        nc.vector.memset(share_of_means[:], -float(PIECE_BANKS * BANK_COLS) / COUNT)
+        share_of_sums = keep.tile([P, P], F32)
+        nc.vector.memset(share_of_sums[:], -1.0 / COUNT)
         identity = keep.tile([P, P], BF16)
         make_identity(nc, identity[:])
 
         def load_weight(j):
-            for half in range(2):
-                cols = slice(half * CHANNELS // 2, (half + 1) * CHANNELS // 2)
+            for piece in range(PIECES):
+                cols = slice(piece * PIECE_TILES * P, (piece + 1) * PIECE_TILES * P)
                 nc.sync.dma_start(out=w_words[:, j, cols].bitcast(I32), in_=words_i32[j, :, cols])
 
         def load_y(u):
@@ -97,10 +96,8 @@ def tile_spatialcgnl_pb_e_kernel(tc, y, Wz_words, Wz_scales, gamma, beta, x, out
         def load_x(u):
             j, b = slabs[u]
             for piece in range(PIECES):
-                first = piece * PIECE_TILES
-                tiles = slice(first, first + PIECE_TILES)
-                rows = slice(j * TILES + first, j * TILES + first + PIECE_TILES)
-                nc.sync.dma_start(out=x_sb[:, u, tiles, :], in_=x_rows[b, :, rows, :])
+                first = j * TILES + piece * PIECE_TILES
+                nc.sync.dma_start(out=x_sb[:, u, piece], in_=x_rows[b, :, first : first + PIECE_TILES, :])
 
         live = GROUPS * BLOCKS_PER_QUADRANT
         for quadrant in range(QUADRANTS):
@@ -125,17 +122,16 @@ def tile_spatialcgnl_pb_e_kernel(tc, y, Wz_words, Wz_scales, gamma, beta, x, out
             nc.tensor.transpose(affine_ps[:], affine_in[:], identity[:])
             nc.vector.tensor_copy(out=affine_cols[:], in_=affine_ps[:, 0 : 2 * affine_rows])
 
-        banks_of = {}
-        neg_mean_of = {}
-        var_of = {}
-        gain_of = {}
-        shift_of = {}
+        banks = {}
+        sums, moments, means, totals, neg_var, rstd, gain, shift = {}, {}, {}, {}, {}, {}, {}, {}
 
-        def quantise(u):
+        def regroup(u):
             nc.vector.tensor_copy(
                 out=y_grouped[:, u].rearrange("p (c i) t -> p c t i", i=4),
                 in_=y_raw[:, u].rearrange("p t (c i) -> p c t i", i=4),
             )
+
+        def quantise(u):
             nc.vector.quantize_mx(
                 out=y_words[:, u, :].bitcast(FP8X4),
                 scales=y_planes[:, u, :],
@@ -144,124 +140,150 @@ def tile_spatialcgnl_pb_e_kernel(tc, y, Wz_words, Wz_scales, gamma, beta, x, out
 
         def multiply(u):
             j = slabs[u][0]
-            banks = []
-            for k in range(BANKS):
-                home = psum_scalar if k < SCALAR_BANKS else psum_vector
-                bank = home.tile([P, TILES_PER_BANK, POSITIONS], F32)
-                for t in range(TILES_PER_BANK):
-                    m = k * TILES_PER_BANK + t
-                    cols = slice(m * P, (m + 1) * P)
-                    nc.tensor.matmul_mx(
-                        out=bank[:, t, :],
-                        lhsT=w_words[:, j, cols].bitcast(FP8X4),
-                        lhsT_scale=w_planes[BLOCKS_PER_QUADRANT * j : P, cols],
-                        rhs=y_words[:, u, :].bitcast(FP8X4),
-                        rhs_scale=y_planes[:, u, :],
-                        start=True,
-                        stop=True,
-                    )
-                banks.append(bank)
-            banks_of[u] = banks
+            for piece in range(PIECES):
+                home = psum_piece0 if piece == 0 else psum_piece1
+                banks[u, piece] = []
+                for k in range(PIECE_BANKS):
+                    bank = home.tile([P, TILES_PER_BANK, POSITIONS], F32)
+                    for t in range(TILES_PER_BANK):
+                        m = piece * PIECE_TILES + k * TILES_PER_BANK + t
+                        cols = slice(m * P, (m + 1) * P)
+                        nc.tensor.matmul_mx(
+                            out=bank[:, t, :],
+                            lhsT=w_words[:, j, cols].bitcast(FP8X4),
+                            lhsT_scale=w_planes[BLOCKS_PER_QUADRANT * j : P, cols],
+                            rhs=y_words[:, u, :].bitcast(FP8X4),
+                            rhs_scale=y_planes[:, u, :],
+                            start=True,
+                            stop=True,
+                        )
+                    banks[u, piece].append(bank)
 
-        def statistics(u):
-            j = slabs[u][0]
-            banks = banks_of[u]
-            sums = small.tile([P, SCALAR_BANKS, 2], F32)
-            for k in range(SCALAR_BANKS):
-                z = banks[k][:].rearrange("p t n -> p (t n)")
+        def sum_piece0(u):
+            sums[u] = small.tile([P, PIECE_BANKS, 2], F32, name="sums")
+            for k in range(PIECE_BANKS):
+                z = banks[u, 0][k][:].rearrange("p t n -> p (t n)")
                 tiles = slice(k * TILES_PER_BANK, (k + 1) * TILES_PER_BANK)
                 nc.scalar.activation(
-                    out=result[:, u, tiles, :].rearrange("p t n -> p (t n)"),
+                    out=result[:, u, 0, tiles, :].rearrange("p t n -> p (t n)"),
                     in_=z,
                     func=ACT.Identity,
-                    accum_out=sums[:, k, 0:1],
+                    accum_out=sums[u][:, k, 0:1],
                 )
                 squares = scratch.tile([P, BANK_COLS], BF16)
-                nc.scalar.activation(out=squares[:], in_=z, func=ACT.Square, accum_out=sums[:, k, 1:2])
-            moments = small.tile([P, VECTOR_BANKS, BN_STATS_DIM], F32)
-            for k in range(VECTOR_BANKS):
-                z = banks[SCALAR_BANKS + k][:].rearrange("p t n -> p (t n)")
-                nc.vector.bn_stats(out=moments[:, k, :], in_=z)
-            means = small.tile([P, 2], F32)
-            nc.vector.bn_aggr(out=means[:], in_=moments[:].rearrange("p k s -> p (k s)"))
+                nc.scalar.activation(out=squares[:], in_=z, func=ACT.Square, accum_out=sums[u][:, k, 1:2])
+
+        def moments_piece1(u):
+            moments[u] = small.tile([P, PIECE_BANKS, BN_STATS_DIM], F32, name="moments")
+            for k in range(PIECE_BANKS):
+                z = banks[u, 1][k][:].rearrange("p t n -> p (t n)")
+                nc.vector.bn_stats(out=moments[u][:, k, :], in_=z)
+
+        def aggregate(u):
+            means[u] = small.tile([P, 2], F32, name="means")
+            nc.vector.bn_aggr(out=means[u][:], in_=moments[u][:].rearrange("p k s -> p (k s)"))
+
+        def second_moment(u):
             nc.vector.scalar_tensor_tensor(
-                out=means[:, 1:2],
-                in0=means[:, 0:1],
-                scalar=means[:, 0:1],
-                in1=means[:, 1:2],
+                out=means[u][:, 1:2],
+                in0=means[u][:, 0:1],
+                scalar=means[u][:, 0:1],
+                in1=means[u][:, 1:2],
                 op0=ALU.mult,
                 op1=ALU.add,
             )
-            totals = psum_small.tile([P, 2], F32, tag="small")
-            nc.tensor.matmul(out=totals[:], lhsT=share_vector[:], rhs=means[:], start=True, stop=False)
-            for k in range(SCALAR_BANKS):
+
+        def add_partitions(u):
+            totals[u] = psum_small.tile([P, 2], F32, tag="small", name="totals")
+            nc.tensor.matmul(out=totals[u][:], lhsT=share_of_means[:], rhs=means[u][:], start=True, stop=False)
+            for k in range(PIECE_BANKS):
                 nc.tensor.matmul(
-                    out=totals[:],
-                    lhsT=share_scalar[:],
-                    rhs=sums[:, k, :],
+                    out=totals[u][:],
+                    lhsT=share_of_sums[:],
+                    rhs=sums[u][:, k, :],
                     start=False,
-                    stop=(k == SCALAR_BANKS - 1),
+                    stop=(k == PIECE_BANKS - 1),
                 )
-            neg_mean = totals[:, 0:1]
-            neg_square = totals[:, 1:2]
-            neg_var = small.tile([P, 1], F32)
-            nc.vector.tensor_scalar(
-                out=neg_var[:], in0=neg_mean, scalar1=neg_mean, scalar2=neg_square, op0=ALU.mult, op1=ALU.add
-            )
-            var = small.tile([P, 1], F32)
-            nc.vector.tensor_scalar(
-                out=var[:], in0=neg_var[:], scalar1=-1.0, scalar2=0.0, op0=ALU.mult, op1=ALU.max
-            )
-            neg_mean_of[u] = neg_mean
-            var_of[u] = var
 
-        def coefficients(u):
+        def variance(u):
+            neg_var[u] = small.tile([P, 1], F32, name="neg_var")
+            nc.vector.tensor_scalar(
+                out=neg_var[u][:],
+                in0=totals[u][:, 0:1],
+                scalar1=totals[u][:, 0:1],
+                scalar2=totals[u][:, 1:2],
+                op0=ALU.mult,
+                op1=ALU.add,
+            )
+
+        def reciprocal_std(u):
+            rstd[u] = small.tile([P, 1], F32, name="rstd")
+            nc.scalar.activation(
+                out=rstd[u][:], in_=neg_var[u][:], func=ACT.Abs_reciprocal_sqrt, scale=-1.0, bias=eps[:]
+            )
+
+        def make_gain(u):
             j = slabs[u][0]
-            std = small.tile([P, 1], F32)
-            nc.scalar.activation(out=std[:], in_=var_of[u][:], func=ACT.Sqrt, bias=eps[:])
-            rstd = small.tile([P, 1], F32)
-            nc.vector.reciprocal(out=rstd[:], in_=std[:])
-            gamma_cols = affine_cols[:, j * TILES : (j + 1) * TILES]
-            beta_cols = affine_cols[:, affine_rows + j * TILES : affine_rows + (j + 1) * TILES]
-            gain = small.tile([P, TILES], F32)
-            nc.vector.tensor_scalar_mul(out=gain[:], in0=gamma_cols, scalar1=rstd[:])
-            shift = small.tile([P, TILES], F32)
-            nc.vector.scalar_tensor_tensor(
-                out=shift[:], in0=gain[:], scalar=neg_mean_of[u], in1=beta_cols, op0=ALU.mult, op1=ALU.add
+            gain[u] = small.tile([P, TILES], F32, name="gain")
+            nc.vector.tensor_scalar_mul(
+                out=gain[u][:], in0=affine_cols[:, j * TILES : (j + 1) * TILES], scalar1=rstd[u][:]
             )
-            gain_of[u] = gain
-            shift_of[u] = shift
 
-        def finish(u):
-            j, b = slabs[u]
-            for piece in reversed(range(PIECES)):
-                first = piece * PIECE_TILES
-                tiles = slice(first, first + PIECE_TILES)
-                for m in range(first, first + PIECE_TILES):
-                    k, t = divmod(m, TILES_PER_BANK)
-                    z = result[:, u, m, :] if k < SCALAR_BANKS else banks_of[u][k][:, t, :]
-                    nc.scalar.activation(
-                        out=result[:, u, m, :],
-                        in_=z,
-                        func=ACT.Identity,
-                        scale=gain_of[u][:, m : m + 1],
-                        bias=shift_of[u][:, m : m + 1],
-                    )
-                nc.vector.tensor_tensor(
-                    out=result[:, u, tiles, :], in0=result[:, u, tiles, :], in1=x_sb[:, u, tiles, :], op=ALU.add
+        def make_shift(u):
+            j = slabs[u][0]
+            shift[u] = small.tile([P, TILES], F32, name="shift")
+            nc.vector.scalar_tensor_tensor(
+                out=shift[u][:],
+                in0=gain[u][:],
+                scalar=totals[u][:, 0:1],
+                in1=affine_cols[:, affine_rows + j * TILES : affine_rows + (j + 1) * TILES],
+                op0=ALU.mult,
+                op1=ALU.add,
+            )
+
+        def normalise(u, piece):
+            for i in range(PIECE_TILES):
+                m = piece * PIECE_TILES + i
+                k, t = divmod(i, TILES_PER_BANK)
+                nc.scalar.activation(
+                    out=result[:, u, piece, i, :],
+                    in_=result[:, u, piece, i, :] if piece == 0 else banks[u, piece][k][:, t, :],
+                    func=ACT.Identity,
+                    scale=gain[u][:, m : m + 1],
+                    bias=shift[u][:, m : m + 1],
                 )
-                rows = slice(j * TILES + first, j * TILES + first + PIECE_TILES)
-                nc.sync.dma_start(out=out_rows[b, :, rows, :], in_=result[:, u, tiles, :])
 
-        quantise(0)
-        spread_affine()
-        quantise(1)
-        for u in range(len(slabs)):
-            multiply(u)
-            statistics(u)
-            if u > 0:
-                finish(u - 1)
-            coefficients(u)
-            if u + AHEAD < len(slabs):
-                quantise(u + AHEAD)
-        finish(len(slabs) - 1)
+        def add_x_and_store(u, piece):
+            j, b = slabs[u]
+            nc.vector.tensor_tensor(
+                out=result[:, u, piece], in0=result[:, u, piece], in1=x_sb[:, u, piece], op=ALU.add
+            )
+            first = j * TILES + piece * PIECE_TILES
+            nc.sync.dma_start(out=out_rows[b, :, first : first + PIECE_TILES, :], in_=result[:, u, piece])
+
+        def do(step, u, *more):
+            if 0 <= u < n_slabs:
+                step(u, *more)
+
+        for u in range(AHEAD):
+            regroup(u)
+            if u == 0:
+                spread_affine()
+            quantise(u)
+        for n in range(n_slabs + 2):
+            do(multiply, n)
+            do(sum_piece0, n)
+            do(moments_piece1, n)
+            do(make_gain, n - 1)
+            do(aggregate, n)
+            do(make_shift, n - 1)
+            do(second_moment, n)
+            do(add_partitions, n)
+            do(normalise, n - 1, 1)
+            do(normalise, n - 1, 0)
+            do(add_x_and_store, n - 2, 0)
+            do(regroup, n + AHEAD)
+            do(variance, n)
+            do(quantise, n + AHEAD)
+            do(reciprocal_std, n)
+            do(add_x_and_store, n - 1, 1)

@@ -31,7 +31,9 @@ QUADRANTS = 4
 BLOCKS_PER_QUADRANT = 4
 BN_STATS_DIM = 6
 COUNT = CHANNELS * POSITIONS
+VECTOR_TILES = 1
 AHEAD = 2
+X_LAG = AHEAD + 1
 
 FLOPS = 2 * IMAGES * GROUPS * CHANNELS * K * POSITIONS
 
@@ -99,21 +101,24 @@ def tile_spatialcgnl_pb_e_kernel(tc, y, Wz_words, Wz_scales, gamma, beta, x, out
                 first = j * TILES + piece * PIECE_TILES
                 nc.sync.dma_start(out=x_sb[:, u, piece], in_=x_rows[b, :, first : first + PIECE_TILES, :])
 
-        live = GROUPS * BLOCKS_PER_QUADRANT
-        for quadrant in range(QUADRANTS):
-            blocks = slice(quadrant * BLOCKS_PER_QUADRANT, (quadrant + 1) * BLOCKS_PER_QUADRANT)
-            nc.sync.dma_start(
-                out=w_planes[:].bitcast(I32)[32 * quadrant : 32 * quadrant + live, :],
-                in_=scales_i32[:, blocks, :],
-            )
-        for j in range(GROUPS):
-            head = j * IMAGES
-            load_y(head)
-            load_weight(j)
-            for u in range(head + 1, head + IMAGES):
+        def load_planes():
+            live = GROUPS * BLOCKS_PER_QUADRANT
+            for quadrant in range(QUADRANTS):
+                blocks = slice(quadrant * BLOCKS_PER_QUADRANT, (quadrant + 1) * BLOCKS_PER_QUADRANT)
+                nc.sync.dma_start(
+                    out=w_planes[:].bitcast(I32)[32 * quadrant : 32 * quadrant + live, :],
+                    in_=scales_i32[:, blocks, :],
+                )
+
+        for u in range(n_slabs + X_LAG):
+            if u < n_slabs:
                 load_y(u)
-            for u in range(head, head + IMAGES):
-                load_x(u)
+                if u == 0:
+                    load_planes()
+                if slabs[u][1] == 0:
+                    load_weight(slabs[u][0])
+            if u >= X_LAG:
+                load_x(u - X_LAG)
 
         affine_cols = keep.tile([P, 2 * affine_rows], F32)
 
@@ -138,40 +143,39 @@ def tile_spatialcgnl_pb_e_kernel(tc, y, Wz_words, Wz_scales, gamma, beta, x, out
                 in_=y_grouped[:, u].rearrange("p n t -> p (n t)"),
             )
 
-        def multiply(u):
+        def multiply(u, piece):
             j = slabs[u][0]
-            for piece in range(PIECES):
-                home = psum_piece0 if piece == 0 else psum_piece1
-                banks[u, piece] = []
-                for k in range(PIECE_BANKS):
-                    bank = home.tile([P, TILES_PER_BANK, POSITIONS], F32)
-                    for t in range(TILES_PER_BANK):
-                        m = piece * PIECE_TILES + k * TILES_PER_BANK + t
-                        cols = slice(m * P, (m + 1) * P)
-                        nc.tensor.matmul_mx(
-                            out=bank[:, t, :],
-                            lhsT=w_words[:, j, cols].bitcast(FP8X4),
-                            lhsT_scale=w_planes[BLOCKS_PER_QUADRANT * j : P, cols],
-                            rhs=y_words[:, u, :].bitcast(FP8X4),
-                            rhs_scale=y_planes[:, u, :],
-                            start=True,
-                            stop=True,
-                        )
-                    banks[u, piece].append(bank)
-
-        def sum_piece0(u):
-            sums[u] = small.tile([P, PIECE_BANKS, 2], F32, name="sums")
+            home = psum_piece0 if piece == 0 else psum_piece1
+            banks[u, piece] = []
             for k in range(PIECE_BANKS):
-                z = banks[u, 0][k][:].rearrange("p t n -> p (t n)")
-                tiles = slice(k * TILES_PER_BANK, (k + 1) * TILES_PER_BANK)
-                nc.scalar.activation(
-                    out=result[:, u, 0, tiles, :].rearrange("p t n -> p (t n)"),
-                    in_=z,
-                    func=ACT.Identity,
-                    accum_out=sums[u][:, k, 0:1],
-                )
-                squares = scratch.tile([P, BANK_COLS], BF16)
-                nc.scalar.activation(out=squares[:], in_=z, func=ACT.Square, accum_out=sums[u][:, k, 1:2])
+                bank = home.tile([P, TILES_PER_BANK, POSITIONS], F32)
+                for t in range(TILES_PER_BANK):
+                    m = piece * PIECE_TILES + k * TILES_PER_BANK + t
+                    cols = slice(m * P, (m + 1) * P)
+                    nc.tensor.matmul_mx(
+                        out=bank[:, t, :],
+                        lhsT=w_words[:, j, cols].bitcast(FP8X4),
+                        lhsT_scale=w_planes[BLOCKS_PER_QUADRANT * j : P, cols],
+                        rhs=y_words[:, u, :].bitcast(FP8X4),
+                        rhs_scale=y_planes[:, u, :],
+                        start=True,
+                        stop=True,
+                    )
+                banks[u, piece].append(bank)
+
+        def sum_bank(u, k):
+            if k == 0:
+                sums[u] = small.tile([P, PIECE_BANKS, 2], F32, name="sums")
+            z = banks[u, 0][k][:].rearrange("p t n -> p (t n)")
+            tiles = slice(k * TILES_PER_BANK, (k + 1) * TILES_PER_BANK)
+            nc.scalar.activation(
+                out=result[:, u, 0, tiles, :].rearrange("p t n -> p (t n)"),
+                in_=z,
+                func=ACT.Identity,
+                accum_out=sums[u][:, k, 0:1],
+            )
+            squares = scratch.tile([P, BANK_COLS], BF16)
+            nc.scalar.activation(out=squares[:], in_=z, func=ACT.Square, accum_out=sums[u][:, k, 1:2])
 
         def moments_piece1(u):
             moments[u] = small.tile([P, PIECE_BANKS, BN_STATS_DIM], F32, name="moments")
@@ -241,8 +245,19 @@ def tile_spatialcgnl_pb_e_kernel(tc, y, Wz_words, Wz_scales, gamma, beta, x, out
                 op1=ALU.add,
             )
 
+        def normalise_on_vector(u):
+            for i in range(VECTOR_TILES):
+                nc.vector.tensor_scalar(
+                    out=result[:, u, 0, i, :],
+                    in0=result[:, u, 0, i, :],
+                    scalar1=gain[u][:, i : i + 1],
+                    scalar2=shift[u][:, i : i + 1],
+                    op0=ALU.mult,
+                    op1=ALU.add,
+                )
+
         def normalise(u, piece):
-            for i in range(PIECE_TILES):
+            for i in range(VECTOR_TILES if piece == 0 else 0, PIECE_TILES):
                 m = piece * PIECE_TILES + i
                 k, t = divmod(i, TILES_PER_BANK)
                 nc.scalar.activation(
@@ -267,23 +282,27 @@ def tile_spatialcgnl_pb_e_kernel(tc, y, Wz_words, Wz_scales, gamma, beta, x, out
 
         for u in range(AHEAD):
             regroup(u)
-            if u == 0:
-                spread_affine()
             quantise(u)
+        multiply(0, 0)
+        multiply(0, 1)
+        spread_affine()
         for n in range(n_slabs + 2):
-            do(multiply, n)
-            do(sum_piece0, n)
+            do(multiply, n + 1, 0)
+            do(sum_bank, n, 0)
+            do(reciprocal_std, n - 1)
+            do(sum_bank, n, 1)
             do(moments_piece1, n)
             do(make_gain, n - 1)
             do(aggregate, n)
             do(make_shift, n - 1)
             do(second_moment, n)
+            do(normalise_on_vector, n - 1)
             do(add_partitions, n)
             do(normalise, n - 1, 1)
+            do(multiply, n + 1, 1)
             do(normalise, n - 1, 0)
             do(add_x_and_store, n - 2, 0)
             do(regroup, n + AHEAD)
             do(variance, n)
             do(quantise, n + AHEAD)
-            do(reciprocal_std, n)
             do(add_x_and_store, n - 1, 1)

@@ -23,17 +23,13 @@ P = 128
 PACK = 4
 TILES = CHANNELS // P
 TILES_PER_BANK = 512 // POSITIONS
+BANKS = TILES // TILES_PER_BANK
 BANK_COLS = TILES_PER_BANK * POSITIONS
-PIECES = 2
-PIECE_TILES = TILES // PIECES
-PIECE_BANKS = PIECE_TILES // TILES_PER_BANK
 QUADRANTS = 4
 BLOCKS_PER_QUADRANT = 4
-BN_STATS_DIM = 6
 COUNT = CHANNELS * POSITIONS
-VECTOR_TILES = 1
-AHEAD = 2
-X_LAG = AHEAD + 1
+LEAD = 2
+HALF = TILES // 2
 
 FLOPS = 2 * IMAGES * GROUPS * CHANNELS * K * POSITIONS
 
@@ -55,10 +51,10 @@ def tile_spatialcgnl_pb_e_kernel(tc, y, Wz_words, Wz_scales, gamma, beta, x, out
     with ExitStack() as ctx:
         ctx.enter_context(tc.manual_schedule())
         keep = ctx.enter_context(tc.tile_pool(name="keep", bufs=1))
-        small = ctx.enter_context(tc.tile_pool(name="small", bufs=3))
-        scratch = ctx.enter_context(tc.tile_pool(name="scratch", bufs=4))
-        psum_piece0 = ctx.enter_context(tc.psum_pool(name="psum_piece0", bufs=PIECE_BANKS + 1))
-        psum_piece1 = ctx.enter_context(tc.psum_pool(name="psum_piece1", bufs=2 * PIECE_BANKS))
+        scratch = ctx.enter_context(tc.tile_pool(name="scratch", bufs=3))
+        psum_stats = ctx.enter_context(tc.psum_pool(name="psum_stats", bufs=3))
+        psum_final = ctx.enter_context(tc.psum_pool(name="psum_final", bufs=3))
+        psum_sigma = ctx.enter_context(tc.psum_pool(name="psum_sigma", bufs=1))
         psum_small = ctx.enter_context(tc.psum_pool(name="psum_small", bufs=1))
 
         w_words = keep.tile([P, GROUPS, CHANNELS], U32, align_bytes=64)
@@ -67,8 +63,14 @@ def tile_spatialcgnl_pb_e_kernel(tc, y, Wz_words, Wz_scales, gamma, beta, x, out
         y_grouped = keep.tile([P, n_slabs, POSITIONS, PACK], BF16, align_bytes=64)
         y_words = keep.tile([P, n_slabs, POSITIONS], U32, align_bytes=64)
         y_planes = keep.tile([P, n_slabs, POSITIONS], U8, align_bytes=64)
-        x_sb = keep.tile([P, n_slabs, PIECES, PIECE_TILES, POSITIONS], BF16)
-        result = keep.tile([P, n_slabs, PIECES, PIECE_TILES, POSITIONS], F32)
+        x_sb = keep.tile([P, n_slabs, TILES, POSITIONS], BF16)
+        x_shifted = keep.tile([P, n_slabs, TILES, POSITIONS], F32)
+        result = keep.tile([P, n_slabs, TILES, POSITIONS], F32)
+        stat = keep.tile([P, n_slabs, 8], F32)
+        neg_var = keep.tile([P, n_slabs], F32)
+        rstd = keep.tile([P, n_slabs], F32)
+        gain = keep.tile([P, n_slabs, TILES], F32)
+        shift = keep.tile([P, n_slabs, TILES], F32)
 
         nc.vector.memset(w_planes[:].bitcast(I32), 0)
         affine_in = keep.tile([P, P], BF16)
@@ -79,16 +81,14 @@ def tile_spatialcgnl_pb_e_kernel(tc, y, Wz_words, Wz_scales, gamma, beta, x, out
         nc.vector.memset(eps[:], EPS)
         warm = keep.tile([P, 1], F32)
         nc.scalar.activation(out=warm[:], in_=eps[:], func=ACT.Abs_reciprocal_sqrt)
-        share_of_means = keep.tile([P, P], F32)
-        nc.vector.memset(share_of_means[:], -float(PIECE_BANKS * BANK_COLS) / COUNT)
-        share_of_sums = keep.tile([P, P], F32)
-        nc.vector.memset(share_of_sums[:], -1.0 / COUNT)
+        share = keep.tile([P, P], F32)
+        nc.vector.memset(share[:], -1.0 / COUNT)
         identity = keep.tile([P, P], BF16)
         make_identity(nc, identity[:])
 
         def load_weight(j):
-            for piece in range(PIECES):
-                cols = slice(piece * PIECE_TILES * P, (piece + 1) * PIECE_TILES * P)
+            for half in range(2):
+                cols = slice(half * HALF * P, (half + 1) * HALF * P)
                 nc.sync.dma_start(out=w_words[:, j, cols].bitcast(I32), in_=words_i32[j, :, cols])
 
         def load_y(u):
@@ -97,9 +97,12 @@ def tile_spatialcgnl_pb_e_kernel(tc, y, Wz_words, Wz_scales, gamma, beta, x, out
 
         def load_x(u):
             j, b = slabs[u]
-            for piece in range(PIECES):
-                first = j * TILES + piece * PIECE_TILES
-                nc.sync.dma_start(out=x_sb[:, u, piece], in_=x_rows[b, :, first : first + PIECE_TILES, :])
+            for half in range(2):
+                first = half * HALF
+                nc.sync.dma_start(
+                    out=x_sb[:, u, first : first + HALF, :],
+                    in_=x_rows[b, :, j * TILES + first : j * TILES + first + HALF, :],
+                )
 
         def load_planes():
             live = GROUPS * BLOCKS_PER_QUADRANT
@@ -110,15 +113,18 @@ def tile_spatialcgnl_pb_e_kernel(tc, y, Wz_words, Wz_scales, gamma, beta, x, out
                     in_=scales_i32[:, blocks, :],
                 )
 
-        for u in range(n_slabs + X_LAG):
-            if u < n_slabs:
-                load_y(u)
-                if u == 0:
-                    load_planes()
-                if slabs[u][1] == 0:
-                    load_weight(slabs[u][0])
-            if u >= X_LAG:
-                load_x(u - X_LAG)
+        load_y(0)
+        load_planes()
+        load_weight(0)
+        load_y(1)
+        load_y(2)
+        load_y(3)
+        load_x(0)
+        load_y(4)
+        load_y(5)
+        load_weight(1)
+        for u in range(1, n_slabs):
+            load_x(u)
 
         affine_cols = keep.tile([P, 2 * affine_rows], F32)
 
@@ -127,8 +133,7 @@ def tile_spatialcgnl_pb_e_kernel(tc, y, Wz_words, Wz_scales, gamma, beta, x, out
             nc.tensor.transpose(affine_ps[:], affine_in[:], identity[:])
             nc.vector.tensor_copy(out=affine_cols[:], in_=affine_ps[:, 0 : 2 * affine_rows])
 
-        banks = {}
-        sums, moments, means, totals, neg_var, rstd, gain, shift = {}, {}, {}, {}, {}, {}, {}, {}
+        stats_banks, final_banks, sigma, totals = {}, {}, {}, {}
 
         def regroup(u):
             nc.vector.tensor_copy(
@@ -143,76 +148,58 @@ def tile_spatialcgnl_pb_e_kernel(tc, y, Wz_words, Wz_scales, gamma, beta, x, out
                 in_=y_grouped[:, u].rearrange("p n t -> p (n t)"),
             )
 
-        def multiply(u, piece):
+        def mx_pass(dest, u, m, start, stop):
             j = slabs[u][0]
-            home = psum_piece0 if piece == 0 else psum_piece1
-            banks[u, piece] = []
-            for k in range(PIECE_BANKS):
-                bank = home.tile([P, TILES_PER_BANK, POSITIONS], F32)
-                for t in range(TILES_PER_BANK):
-                    m = piece * PIECE_TILES + k * TILES_PER_BANK + t
-                    cols = slice(m * P, (m + 1) * P)
-                    nc.tensor.matmul_mx(
-                        out=bank[:, t, :],
-                        lhsT=w_words[:, j, cols].bitcast(FP8X4),
-                        lhsT_scale=w_planes[BLOCKS_PER_QUADRANT * j : P, cols],
-                        rhs=y_words[:, u, :].bitcast(FP8X4),
-                        rhs_scale=y_planes[:, u, :],
-                        start=True,
-                        stop=True,
-                    )
-                banks[u, piece].append(bank)
-
-        def sum_bank(u, k):
-            if k == 0:
-                sums[u] = small.tile([P, PIECE_BANKS, 2], F32, name="sums")
-            z = banks[u, 0][k][:].rearrange("p t n -> p (t n)")
-            tiles = slice(k * TILES_PER_BANK, (k + 1) * TILES_PER_BANK)
-            nc.scalar.activation(
-                out=result[:, u, 0, tiles, :].rearrange("p t n -> p (t n)"),
-                in_=z,
-                func=ACT.Identity,
-                accum_out=sums[u][:, k, 0:1],
+            cols = slice(m * P, (m + 1) * P)
+            nc.tensor.matmul_mx(
+                out=dest,
+                lhsT=w_words[:, j, cols].bitcast(FP8X4),
+                lhsT_scale=w_planes[BLOCKS_PER_QUADRANT * j : P, cols],
+                rhs=y_words[:, u, :].bitcast(FP8X4),
+                rhs_scale=y_planes[:, u, :],
+                start=start,
+                stop=stop,
             )
+
+        def stats_bank(u, k):
+            zs = psum_stats.tile([P, TILES_PER_BANK, POSITIONS], F32)
+            for t in range(TILES_PER_BANK):
+                mx_pass(zs[:, t, :], u, k * TILES_PER_BANK + t, True, True)
+            stats_banks[u, k] = zs
+
+        def sigma_passes(u, first, last):
+            if first == 0:
+                sg = psum_sigma.tile([P, BANK_COLS], F32)
+                sigma[u] = sg
+            for m in range(first, last):
+                mx_pass(sigma[u][:, 0:POSITIONS], u, m, m == 0, m == TILES - 1)
+
+        def square(u, k):
             squares = scratch.tile([P, BANK_COLS], BF16)
-            nc.scalar.activation(out=squares[:], in_=z, func=ACT.Square, accum_out=sums[u][:, k, 1:2])
-
-        def moments_piece1(u):
-            moments[u] = small.tile([P, PIECE_BANKS, BN_STATS_DIM], F32, name="moments")
-            for k in range(PIECE_BANKS):
-                z = banks[u, 1][k][:].rearrange("p t n -> p (t n)")
-                nc.vector.bn_stats(out=moments[u][:, k, :], in_=z)
-
-        def aggregate(u):
-            means[u] = small.tile([P, 2], F32, name="means")
-            nc.vector.bn_aggr(out=means[u][:], in_=moments[u][:].rearrange("p k s -> p (k s)"))
-
-        def second_moment(u):
-            nc.vector.scalar_tensor_tensor(
-                out=means[u][:, 1:2],
-                in0=means[u][:, 0:1],
-                scalar=means[u][:, 0:1],
-                in1=means[u][:, 1:2],
-                op0=ALU.mult,
-                op1=ALU.add,
+            nc.scalar.activation(
+                out=squares[:],
+                in_=stats_banks[u, k][:].rearrange("p t n -> p (t n)"),
+                func=ACT.Square,
+                accum_out=stat[:, u, k : k + 1],
             )
+
+        def sigma_sum(u):
+            copied = scratch.tile([P, POSITIONS], BF16)
+            nc.scalar.activation(
+                out=copied[:], in_=sigma[u][:, 0:POSITIONS], func=ACT.Identity, accum_out=stat[:, u, 4:5]
+            )
+
+        def join_squares(u):
+            four = scratch.tile([P, BANKS], F32)
+            nc.scalar.activation(out=four[:], in_=stat[:, u, 0:BANKS], func=ACT.Identity, accum_out=stat[:, u, 5:6])
 
         def add_partitions(u):
             totals[u] = psum_small.tile([P, 2], F32, tag="small", name="totals")
-            nc.tensor.matmul(out=totals[u][:], lhsT=share_of_means[:], rhs=means[u][:], start=True, stop=False)
-            for k in range(PIECE_BANKS):
-                nc.tensor.matmul(
-                    out=totals[u][:],
-                    lhsT=share_of_sums[:],
-                    rhs=sums[u][:, k, :],
-                    start=False,
-                    stop=(k == PIECE_BANKS - 1),
-                )
+            nc.tensor.matmul(out=totals[u][:], lhsT=share[:], rhs=stat[:, u, 4:6], start=True, stop=True)
 
         def variance(u):
-            neg_var[u] = small.tile([P, 1], F32, name="neg_var")
             nc.vector.tensor_scalar(
-                out=neg_var[u][:],
+                out=neg_var[:, u : u + 1],
                 in0=totals[u][:, 0:1],
                 scalar1=totals[u][:, 0:1],
                 scalar2=totals[u][:, 1:2],
@@ -221,88 +208,136 @@ def tile_spatialcgnl_pb_e_kernel(tc, y, Wz_words, Wz_scales, gamma, beta, x, out
             )
 
         def reciprocal_std(u):
-            rstd[u] = small.tile([P, 1], F32, name="rstd")
             nc.scalar.activation(
-                out=rstd[u][:], in_=neg_var[u][:], func=ACT.Abs_reciprocal_sqrt, scale=-1.0, bias=eps[:]
+                out=rstd[:, u : u + 1],
+                in_=neg_var[:, u : u + 1],
+                func=ACT.Abs_reciprocal_sqrt,
+                scale=-1.0,
+                bias=eps[:],
             )
 
         def make_gain(u):
             j = slabs[u][0]
-            gain[u] = small.tile([P, TILES], F32, name="gain")
             nc.vector.tensor_scalar_mul(
-                out=gain[u][:], in0=affine_cols[:, j * TILES : (j + 1) * TILES], scalar1=rstd[u][:]
+                out=gain[:, u, :], in0=affine_cols[:, j * TILES : (j + 1) * TILES], scalar1=rstd[:, u : u + 1]
             )
 
         def make_shift(u):
             j = slabs[u][0]
-            shift[u] = small.tile([P, TILES], F32, name="shift")
             nc.vector.scalar_tensor_tensor(
-                out=shift[u][:],
-                in0=gain[u][:],
+                out=shift[:, u, :],
+                in0=gain[:, u, :],
                 scalar=totals[u][:, 0:1],
                 in1=affine_cols[:, affine_rows + j * TILES : affine_rows + (j + 1) * TILES],
                 op0=ALU.mult,
                 op1=ALU.add,
             )
 
-        def normalise_on_vector(u):
-            for i in range(VECTOR_TILES):
-                nc.vector.tensor_scalar(
-                    out=result[:, u, 0, i, :],
-                    in0=result[:, u, 0, i, :],
-                    scalar1=gain[u][:, i : i + 1],
-                    scalar2=shift[u][:, i : i + 1],
+        def shift_x(u, m, on_scalar):
+            if on_scalar:
+                nc.scalar.activation(
+                    out=x_shifted[:, u, m, :],
+                    in_=x_sb[:, u, m, :],
+                    func=ACT.Identity,
+                    bias=shift[:, u, m : m + 1],
+                )
+            else:
+                nc.gpsimd.tensor_scalar(
+                    out=x_shifted[:, u, m, :],
+                    in0=x_sb[:, u, m, :],
+                    scalar1=1.0,
+                    scalar2=shift[:, u, m : m + 1],
                     op0=ALU.mult,
                     op1=ALU.add,
                 )
 
-        def normalise(u, piece):
-            for i in range(VECTOR_TILES if piece == 0 else 0, PIECE_TILES):
-                m = piece * PIECE_TILES + i
-                k, t = divmod(i, TILES_PER_BANK)
-                nc.scalar.activation(
-                    out=result[:, u, piece, i, :],
-                    in_=result[:, u, piece, i, :] if piece == 0 else banks[u, piece][k][:, t, :],
-                    func=ACT.Identity,
-                    scale=gain[u][:, m : m + 1],
-                    bias=shift[u][:, m : m + 1],
+        def shift_x_all(u):
+            for m in range(TILES):
+                shift_x(u, m, u == n_slabs - 1 and m % 2 == 1)
+
+        def final_bank(u, k):
+            zf = psum_final.tile([P, TILES_PER_BANK, POSITIONS], F32)
+            for t in range(TILES_PER_BANK):
+                mx_pass(zf[:, t, :], u, k * TILES_PER_BANK + t, True, True)
+            final_banks[u, k] = zf
+
+        def finish(u, k):
+            for t in range(TILES_PER_BANK):
+                m = k * TILES_PER_BANK + t
+                nc.vector.scalar_tensor_tensor(
+                    out=result[:, u, m, :],
+                    in0=final_banks[u, k][:, t, :],
+                    scalar=gain[:, u, m : m + 1],
+                    in1=x_shifted[:, u, m, :],
+                    op0=ALU.mult,
+                    op1=ALU.add,
                 )
 
-        def add_x_and_store(u, piece):
+        def store(u, first, count):
             j, b = slabs[u]
-            nc.vector.tensor_tensor(
-                out=result[:, u, piece], in0=result[:, u, piece], in1=x_sb[:, u, piece], op=ALU.add
+            nc.sync.dma_start(
+                out=out_rows[b, :, j * TILES + first : j * TILES + first + count, :],
+                in_=result[:, u, first : first + count, :],
             )
-            first = j * TILES + piece * PIECE_TILES
-            nc.sync.dma_start(out=out_rows[b, :, first : first + PIECE_TILES, :], in_=result[:, u, piece])
 
         def do(step, u, *more):
             if 0 <= u < n_slabs:
                 step(u, *more)
 
-        for u in range(AHEAD):
-            regroup(u)
-            quantise(u)
-        multiply(0, 0)
-        multiply(0, 1)
-        spread_affine()
-        for n in range(n_slabs + 2):
-            do(multiply, n + 1, 0)
-            do(sum_bank, n, 0)
-            do(reciprocal_std, n - 1)
-            do(sum_bank, n, 1)
-            do(moments_piece1, n)
-            do(make_gain, n - 1)
-            do(aggregate, n)
-            do(make_shift, n - 1)
-            do(second_moment, n)
-            do(normalise_on_vector, n - 1)
-            do(add_partitions, n)
-            do(normalise, n - 1, 1)
-            do(multiply, n + 1, 1)
-            do(normalise, n - 1, 0)
-            do(add_x_and_store, n - 2, 0)
-            do(regroup, n + AHEAD)
-            do(variance, n)
-            do(quantise, n + AHEAD)
-            do(add_x_and_store, n - 1, 1)
+        regroup(0)
+        quantise(0)
+        for r in range(-LEAD, n_slabs):
+            s, c, f = r + LEAD, r + LEAD - 1, r
+            last = f == n_slabs - 1
+            do(stats_bank, s, 0)
+            do(sigma_passes, s, 0, HALF)
+            do(square, s, 0)
+            do(add_partitions, c)
+            do(final_bank, f, 0)
+            do(finish, f, 0)
+            if last:
+                store(f, 0, 2)
+            do(stats_bank, s, 1)
+            do(sigma_passes, s, HALF, TILES)
+            do(square, s, 1)
+            if r == -LEAD:
+                spread_affine()
+                regroup(1)
+                regroup(2)
+                quantise(1)
+                regroup(3)
+                quantise(2)
+            do(variance, c)
+            if r == -LEAD + 1:
+                regroup(4)
+                quantise(3)
+            do(final_bank, f, 1)
+            do(finish, f, 1)
+            if last:
+                store(f, 2, 2)
+            else:
+                do(store, f, 0, HALF)
+            do(sigma_sum, s)
+            do(reciprocal_std, c)
+            do(stats_bank, s, 2)
+            do(square, s, 2)
+            do(make_gain, c)
+            do(make_shift, c)
+            do(shift_x_all, c)
+            if r == -LEAD + 1:
+                regroup(5)
+                quantise(4)
+                quantise(5)
+            do(final_bank, f, 2)
+            do(finish, f, 2)
+            if last:
+                store(f, 4, 2)
+            do(stats_bank, s, 3)
+            do(square, s, 3)
+            do(join_squares, s)
+            do(final_bank, f, 3)
+            do(finish, f, 3)
+            if last:
+                store(f, 6, 2)
+            else:
+                do(store, f, HALF, HALF)

@@ -233,8 +233,16 @@ def tile_spatialcgnl_pb_e_kernel(tc, y, Wz_words, Wz_scales, gamma, beta, x, out
                 op1=ALU.add,
             )
 
-        def shift_x(u, m, on_scalar):
-            if on_scalar:
+        def shift_x(u, m, owner):
+            if owner == "V":
+                nc.vector.tensor_scalar(
+                    out=x_shifted[:, u, m, :],
+                    in0=x_sb[:, u, m, :],
+                    scalar1=shift[:, u, m : m + 1],
+                    scalar2=None,
+                    op0=ALU.add,
+                )
+            elif owner == "S":
                 nc.scalar.activation(
                     out=x_shifted[:, u, m, :],
                     in_=x_sb[:, u, m, :],
@@ -251,9 +259,11 @@ def tile_spatialcgnl_pb_e_kernel(tc, y, Wz_words, Wz_scales, gamma, beta, x, out
                     op1=ALU.add,
                 )
 
-        def shift_x_all(u):
+        def shift_x_by(u, owner):
+            owners = "VSGSGSGS" if u == n_slabs - 1 else "VGGGSGGV"
             for m in range(TILES):
-                shift_x(u, m, u == n_slabs - 1 and m % 2 == 1)
+                if owners[m] == owner:
+                    shift_x(u, m, owner)
 
         def final_bank(u, k):
             zf = psum_final.tile([P, TILES_PER_BANK, POSITIONS], F32)
@@ -323,7 +333,7 @@ def tile_spatialcgnl_pb_e_kernel(tc, y, Wz_words, Wz_scales, gamma, beta, x, out
             do(square, s, 2)
             do(make_gain, c)
             do(make_shift, c)
-            do(shift_x_all, c)
+            do(shift_x_by, c, "G")
             if r == -LEAD + 1:
                 regroup(5)
                 quantise(4)
@@ -332,9 +342,11 @@ def tile_spatialcgnl_pb_e_kernel(tc, y, Wz_words, Wz_scales, gamma, beta, x, out
             do(finish, f, 2)
             if last:
                 store(f, 4, 2)
+            do(shift_x_by, c, "V")
             do(stats_bank, s, 3)
             do(square, s, 3)
             do(join_squares, s)
+            do(shift_x_by, c, "S")
             do(final_bank, f, 3)
             do(finish, f, 3)
             if last:

@@ -69,6 +69,7 @@ def tile_spatialcgnl_pb_e_kernel(tc, y, Wz_words, Wz_scales, gamma, beta, x, out
         stat = keep.tile([P, n_slabs, 8], F32)
         neg_var = keep.tile([P, n_slabs], F32)
         rstd = keep.tile([P, n_slabs], F32)
+        neg_mean_over_std = keep.tile([P, n_slabs], F32)
         gain = keep.tile([P, n_slabs, TILES], F32)
         shift = keep.tile([P, n_slabs, TILES], F32)
 
@@ -119,18 +120,20 @@ def tile_spatialcgnl_pb_e_kernel(tc, y, Wz_words, Wz_scales, gamma, beta, x, out
         load_y(1)
         load_y(2)
         load_y(3)
-        load_x(0)
         load_y(4)
         load_y(5)
+        load_x(0)
         load_weight(1)
         for u in range(1, n_slabs):
             load_x(u)
 
         affine_cols = keep.tile([P, 2 * affine_rows], F32)
 
+        small_bank = psum_small.tile([P, BANK_COLS], F32)
+        affine_ps = small_bank[:, BANK_COLS // 2 : BANK_COLS // 2 + P // 2].bitcast(BF16)
+
         def spread_affine():
-            affine_ps = psum_small.tile([P, P], BF16, tag="small")
-            nc.tensor.transpose(affine_ps[:], affine_in[:], identity[:])
+            nc.tensor.transpose(affine_ps, affine_in[:], identity[:])
             nc.vector.tensor_copy(out=affine_cols[:], in_=affine_ps[:, 0 : 2 * affine_rows])
 
         stats_banks, final_banks, sigma, totals = {}, {}, {}, {}
@@ -194,8 +197,8 @@ def tile_spatialcgnl_pb_e_kernel(tc, y, Wz_words, Wz_scales, gamma, beta, x, out
             nc.scalar.activation(out=four[:], in_=stat[:, u, 0:BANKS], func=ACT.Identity, accum_out=stat[:, u, 5:6])
 
         def add_partitions(u):
-            totals[u] = psum_small.tile([P, 2], F32, tag="small", name="totals")
-            nc.tensor.matmul(out=totals[u][:], lhsT=share[:], rhs=stat[:, u, 4:6], start=True, stop=True)
+            totals[u] = small_bank[:, 2 * u : 2 * u + 2]
+            nc.tensor.matmul(out=totals[u], lhsT=share[:], rhs=stat[:, u, 4:6], start=True, stop=True)
 
         def variance(u):
             nc.vector.tensor_scalar(
@@ -219,15 +222,20 @@ def tile_spatialcgnl_pb_e_kernel(tc, y, Wz_words, Wz_scales, gamma, beta, x, out
         def make_gain(u):
             j = slabs[u][0]
             nc.vector.tensor_scalar_mul(
-                out=gain[:, u, :], in0=affine_cols[:, j * TILES : (j + 1) * TILES], scalar1=rstd[:, u : u + 1]
+                out=gain[:, u, :], in0=affine_ps[:, j * TILES : (j + 1) * TILES], scalar1=rstd[:, u : u + 1]
+            )
+
+        def make_neg_mean_over_std(u):
+            nc.vector.tensor_scalar_mul(
+                out=neg_mean_over_std[:, u : u + 1], in0=totals[u][:, 0:1], scalar1=rstd[:, u : u + 1]
             )
 
         def make_shift(u):
             j = slabs[u][0]
             nc.vector.scalar_tensor_tensor(
                 out=shift[:, u, :],
-                in0=gain[:, u, :],
-                scalar=totals[u][:, 0:1],
+                in0=affine_ps[:, j * TILES : (j + 1) * TILES],
+                scalar=neg_mean_over_std[:, u : u + 1],
                 in1=affine_cols[:, affine_rows + j * TILES : affine_rows + (j + 1) * TILES],
                 op0=ALU.mult,
                 op1=ALU.add,
@@ -260,7 +268,7 @@ def tile_spatialcgnl_pb_e_kernel(tc, y, Wz_words, Wz_scales, gamma, beta, x, out
                 )
 
         def shift_x_by(u, owner):
-            owners = "VSGSGSGS" if u == n_slabs - 1 else "VGGGSGGV"
+            owners = "SGSGSGSG" if u == n_slabs - 1 else "SGGGSGGG"
             for m in range(TILES):
                 if owners[m] == owner:
                     shift_x(u, m, owner)
@@ -317,10 +325,12 @@ def tile_spatialcgnl_pb_e_kernel(tc, y, Wz_words, Wz_scales, gamma, beta, x, out
                 quantise(1)
                 regroup(3)
                 quantise(2)
-            do(variance, c)
-            if r == -LEAD + 1:
                 regroup(4)
                 quantise(3)
+                regroup(5)
+                quantise(4)
+                quantise(5)
+            do(variance, c)
             do(final_bank, f, 1)
             do(finish, f, 1)
             if last:
@@ -331,18 +341,14 @@ def tile_spatialcgnl_pb_e_kernel(tc, y, Wz_words, Wz_scales, gamma, beta, x, out
             do(reciprocal_std, c)
             do(stats_bank, s, 2)
             do(square, s, 2)
+            do(make_neg_mean_over_std, c)
             do(make_gain, c)
             do(make_shift, c)
             do(shift_x_by, c, "G")
-            if r == -LEAD + 1:
-                regroup(5)
-                quantise(4)
-                quantise(5)
             do(final_bank, f, 2)
             do(finish, f, 2)
             if last:
                 store(f, 4, 2)
-            do(shift_x_by, c, "V")
             do(stats_bank, s, 3)
             do(square, s, 3)
             do(join_squares, s)

@@ -30,6 +30,8 @@ BLOCKS_PER_QUADRANT = 4
 COUNT = CHANNELS * POSITIONS
 LEAD = 2
 HALF = TILES // 2
+BN_STATS_DIM = 6
+VECTOR_BANKS = (2, 3)
 
 FLOPS = 2 * IMAGES * GROUPS * CHANNELS * K * POSITIONS
 
@@ -84,13 +86,16 @@ def tile_spatialcgnl_pb_e_kernel(tc, y, Wz_words, Wz_scales, gamma, beta, x, out
         nc.scalar.activation(out=warm[:], in_=eps[:], func=ACT.Abs_reciprocal_sqrt)
         share = keep.tile([P, P], F32)
         nc.vector.memset(share[:], -1.0 / COUNT)
+        share_of_means = keep.tile([P, P], F32)
+        nc.vector.memset(share_of_means[:], -float(len(VECTOR_BANKS) * BANK_COLS) / COUNT)
+        moments = keep.tile([P, len(VECTOR_BANKS), BN_STATS_DIM], F32)
+        means = keep.tile([P, 2], F32)
         identity = keep.tile([P, P], BF16)
         make_identity(nc, identity[:])
 
-        def load_weight(j):
-            for half in range(2):
-                cols = slice(half * HALF * P, (half + 1) * HALF * P)
-                nc.sync.dma_start(out=w_words[:, j, cols].bitcast(I32), in_=words_i32[j, :, cols])
+        def load_weight(j, half):
+            cols = slice(half * HALF * P, (half + 1) * HALF * P)
+            nc.sync.dma_start(out=w_words[:, j, cols].bitcast(I32), in_=words_i32[j, :, cols])
 
         def load_y(u):
             j, b = slabs[u]
@@ -116,15 +121,19 @@ def tile_spatialcgnl_pb_e_kernel(tc, y, Wz_words, Wz_scales, gamma, beta, x, out
 
         load_y(0)
         load_planes()
-        load_weight(0)
+        load_weight(0, 0)
         load_y(1)
+        load_weight(0, 1)
         load_y(2)
-        load_y(3)
-        load_y(4)
-        load_y(5)
         load_x(0)
-        load_weight(1)
-        for u in range(1, n_slabs):
+        load_y(3)
+        load_x(1)
+        load_weight(1, 0)
+        load_weight(1, 1)
+        load_y(4)
+        load_x(2)
+        load_y(5)
+        for u in range(3, n_slabs):
             load_x(u)
 
         affine_cols = keep.tile([P, 2 * affine_rows], F32)
@@ -170,12 +179,33 @@ def tile_spatialcgnl_pb_e_kernel(tc, y, Wz_words, Wz_scales, gamma, beta, x, out
                 mx_pass(zs[:, t, :], u, k * TILES_PER_BANK + t, True, True)
             stats_banks[u, k] = zs
 
+        def scalar_tiles(u):
+            return HALF if u == 0 else TILES
+
         def sigma_passes(u, first, last):
             if first == 0:
                 sg = psum_sigma.tile([P, BANK_COLS], F32)
                 sigma[u] = sg
             for m in range(first, last):
-                mx_pass(sigma[u][:, 0:POSITIONS], u, m, m == 0, m == TILES - 1)
+                mx_pass(sigma[u][:, 0:POSITIONS], u, m, m == 0, m == scalar_tiles(u) - 1)
+
+        def moments_of(u, k):
+            nc.vector.bn_stats(
+                out=moments[:, VECTOR_BANKS.index(k), :], in_=final_banks[u, k][:].rearrange("p t n -> p (t n)")
+            )
+
+        def aggregate():
+            nc.vector.bn_aggr(out=means[:], in_=moments[:].rearrange("p k s -> p (k s)"))
+
+        def second_moment():
+            nc.vector.scalar_tensor_tensor(
+                out=means[:, 1:2],
+                in0=means[:, 0:1],
+                scalar=means[:, 0:1],
+                in1=means[:, 1:2],
+                op0=ALU.mult,
+                op1=ALU.add,
+            )
 
         def square(u, k):
             squares = scratch.tile([P, BANK_COLS], BF16)
@@ -194,11 +224,14 @@ def tile_spatialcgnl_pb_e_kernel(tc, y, Wz_words, Wz_scales, gamma, beta, x, out
 
         def join_squares(u):
             four = scratch.tile([P, BANKS], F32)
-            nc.scalar.activation(out=four[:], in_=stat[:, u, 0:BANKS], func=ACT.Identity, accum_out=stat[:, u, 5:6])
+            n = scalar_tiles(u) // TILES_PER_BANK
+            nc.scalar.activation(out=four[:, 0:n], in_=stat[:, u, 0:n], func=ACT.Identity, accum_out=stat[:, u, 5:6])
 
         def add_partitions(u):
             totals[u] = small_bank[:, 2 * u : 2 * u + 2]
-            nc.tensor.matmul(out=totals[u], lhsT=share[:], rhs=stat[:, u, 4:6], start=True, stop=True)
+            if u == 0:
+                nc.tensor.matmul(out=totals[u], lhsT=share_of_means[:], rhs=means[:], start=True, stop=False)
+            nc.tensor.matmul(out=totals[u], lhsT=share[:], rhs=stat[:, u, 4:6], start=(u != 0), stop=True)
 
         def variance(u):
             nc.vector.tensor_scalar(
@@ -267,13 +300,19 @@ def tile_spatialcgnl_pb_e_kernel(tc, y, Wz_words, Wz_scales, gamma, beta, x, out
                     op1=ALU.add,
                 )
 
+        def final_order(u):
+            return (2, 3, 0, 1) if u == 0 else (0, 1, 2, 3)
+
         def shift_x_by(u, owner):
-            owners = "SGSGSGSG" if u == n_slabs - 1 else "SGGGSGGG"
-            for m in range(TILES):
-                if owners[m] == owner:
-                    shift_x(u, m, owner)
+            owners = "GGSGVVGS" if u == 0 else "SGSGSGSG" if u == n_slabs - 1 else "SGGGSGGG"
+            for k in final_order(u):
+                for m in range(k * TILES_PER_BANK, (k + 1) * TILES_PER_BANK):
+                    if owners[m] == owner:
+                        shift_x(u, m, owner)
 
         def final_bank(u, k):
+            if (u, k) in final_banks:
+                return
             zf = psum_final.tile([P, TILES_PER_BANK, POSITIONS], F32)
             for t in range(TILES_PER_BANK):
                 mx_pass(zf[:, t, :], u, k * TILES_PER_BANK + t, True, True)
@@ -302,60 +341,67 @@ def tile_spatialcgnl_pb_e_kernel(tc, y, Wz_words, Wz_scales, gamma, beta, x, out
             if 0 <= u < n_slabs:
                 step(u, *more)
 
+        def final_step(u, i):
+            if not 0 <= u < n_slabs:
+                return
+            k = final_order(u)[i]
+            final_bank(u, k)
+            finish(u, k)
+            if u == n_slabs - 1:
+                store(u, k * TILES_PER_BANK, TILES_PER_BANK)
+            elif i % 2 == 1:
+                store(u, (k - 1) * TILES_PER_BANK, HALF)
+
         regroup(0)
+        spread_affine()
         quantise(0)
-        for r in range(-LEAD, n_slabs):
+        stats_bank(0, 0)
+        stats_bank(0, 1)
+        final_bank(0, 2)
+        final_bank(0, 3)
+        sigma_passes(0, 0, HALF)
+        regroup(1)
+        square(0, 0)
+        square(0, 1)
+        quantise(1)
+        moments_of(0, 2)
+        moments_of(0, 3)
+        aggregate()
+        second_moment()
+        sigma_sum(0)
+        join_squares(0)
+        for r in range(-1, n_slabs):
             s, c, f = r + LEAD, r + LEAD - 1, r
-            last = f == n_slabs - 1
             do(stats_bank, s, 0)
             do(sigma_passes, s, 0, HALF)
             do(square, s, 0)
             do(add_partitions, c)
-            do(final_bank, f, 0)
-            do(finish, f, 0)
-            if last:
-                store(f, 0, 2)
+            final_step(f, 0)
+            do(regroup, r + 3)
+            do(variance, c)
+            if c == 0:
+                reciprocal_std(c)
             do(stats_bank, s, 1)
             do(sigma_passes, s, HALF, TILES)
             do(square, s, 1)
-            if r == -LEAD:
-                spread_affine()
-                regroup(1)
-                regroup(2)
-                quantise(1)
-                regroup(3)
-                quantise(2)
-                regroup(4)
-                quantise(3)
-                regroup(5)
-                quantise(4)
-                quantise(5)
-            do(variance, c)
-            do(final_bank, f, 1)
-            do(finish, f, 1)
-            if last:
-                store(f, 2, 2)
-            else:
-                do(store, f, 0, HALF)
+            if c != 0:
+                do(reciprocal_std, c)
+            final_step(f, 1)
+            do(quantise, r + 3)
             do(sigma_sum, s)
-            do(reciprocal_std, c)
             do(stats_bank, s, 2)
             do(square, s, 2)
             do(make_neg_mean_over_std, c)
             do(make_gain, c)
             do(make_shift, c)
+            do(shift_x_by, c, "V")
             do(shift_x_by, c, "G")
-            do(final_bank, f, 2)
-            do(finish, f, 2)
-            if last:
-                store(f, 4, 2)
+            if c == 0:
+                shift_x_by(c, "S")
+            final_step(f, 2)
             do(stats_bank, s, 3)
             do(square, s, 3)
             do(join_squares, s)
-            do(shift_x_by, c, "S")
-            do(final_bank, f, 3)
-            do(finish, f, 3)
-            if last:
-                store(f, 6, 2)
-            else:
-                do(store, f, HALF, HALF)
+            if c != 0:
+                do(shift_x_by, c, "S")
+            final_step(f, 3)

@@ -31,6 +31,9 @@ COUNT = CHANNELS * POSITIONS
 LEAD = 2
 HALF = TILES // 2
 BN_STATS_DIM = 6
+OWNERS = ("GGVGVVGG", "VGGGVGGG", "VGGGVGGG", "VGGGVGGG", "SGSGSGSG", "SGSGSGSS")
+WARM_MATMULS = 5
+REGROUPED_BY_GPSIMD = (2, 3)
 VECTOR_BANKS = (2, 3)
 
 FLOPS = 2 * IMAGES * GROUPS * CHANNELS * K * POSITIONS
@@ -92,6 +95,11 @@ def tile_spatialcgnl_pb_e_kernel(tc, y, Wz_words, Wz_scales, gamma, beta, x, out
         means = keep.tile([P, 2], F32)
         identity = keep.tile([P, P], BF16)
         make_identity(nc, identity[:])
+        warm_rhs = keep.tile([P, BANK_COLS], BF16)
+        nc.vector.memset(warm_rhs[:], 0.0)
+        warm_ps = psum_sigma.tile([P, BANK_COLS], F32, tag="sigma")
+        for i in range(WARM_MATMULS):
+            nc.tensor.matmul(out=warm_ps[:], lhsT=identity[:], rhs=warm_rhs[:], start=True, stop=True)
 
         def load_weight(j, half):
             cols = slice(half * HALF * P, (half + 1) * HALF * P)
@@ -125,15 +133,14 @@ def tile_spatialcgnl_pb_e_kernel(tc, y, Wz_words, Wz_scales, gamma, beta, x, out
         load_y(1)
         load_weight(0, 1)
         load_y(2)
-        load_x(0)
         load_y(3)
+        load_y(4)
+        load_x(0)
+        load_y(5)
         load_x(1)
         load_weight(1, 0)
         load_weight(1, 1)
-        load_y(4)
-        load_x(2)
-        load_y(5)
-        for u in range(3, n_slabs):
+        for u in range(2, n_slabs):
             load_x(u)
 
         affine_cols = keep.tile([P, 2 * affine_rows], F32)
@@ -148,10 +155,20 @@ def tile_spatialcgnl_pb_e_kernel(tc, y, Wz_words, Wz_scales, gamma, beta, x, out
         stats_banks, final_banks, sigma, totals = {}, {}, {}, {}
 
         def regroup(u):
-            nc.vector.tensor_copy(
-                out=y_grouped[:, u].rearrange("p (c i) t -> p c t i", i=4),
-                in_=y_raw[:, u].rearrange("p t (c i) -> p c t i", i=4),
-            )
+            if u in REGROUPED_BY_GPSIMD:
+                nc.gpsimd.tensor_scalar(
+                    out=y_grouped[:, u],
+                    in0=y_raw[:, u].rearrange("p t n -> p n t"),
+                    scalar1=1.0,
+                    scalar2=0.0,
+                    op0=ALU.mult,
+                    op1=ALU.add,
+                )
+            else:
+                nc.vector.tensor_copy(
+                    out=y_grouped[:, u].rearrange("p (c i) t -> p c t i", i=4),
+                    in_=y_raw[:, u].rearrange("p t (c i) -> p c t i", i=4),
+                )
 
         def quantise(u):
             nc.vector.quantize_mx(
@@ -184,7 +201,7 @@ def tile_spatialcgnl_pb_e_kernel(tc, y, Wz_words, Wz_scales, gamma, beta, x, out
 
         def sigma_passes(u, first, last):
             if first == 0:
-                sg = psum_sigma.tile([P, BANK_COLS], F32)
+                sg = psum_sigma.tile([P, BANK_COLS], F32, tag="sigma")
                 sigma[u] = sg
             for m in range(first, last):
                 mx_pass(sigma[u][:, 0:POSITIONS], u, m, m == 0, m == scalar_tiles(u) - 1)
@@ -304,7 +321,7 @@ def tile_spatialcgnl_pb_e_kernel(tc, y, Wz_words, Wz_scales, gamma, beta, x, out
             return (2, 3, 0, 1) if u == 0 else (0, 1, 2, 3)
 
         def shift_x_by(u, owner):
-            owners = "GGSGVVGS" if u == 0 else "SGSGSGSG" if u == n_slabs - 1 else "SGGGSGGG"
+            owners = OWNERS[u]
             for k in final_order(u):
                 for m in range(k * TILES_PER_BANK, (k + 1) * TILES_PER_BANK):
                     if owners[m] == owner:
@@ -361,6 +378,8 @@ def tile_spatialcgnl_pb_e_kernel(tc, y, Wz_words, Wz_scales, gamma, beta, x, out
         final_bank(0, 3)
         sigma_passes(0, 0, HALF)
         regroup(1)
+        regroup(2)
+        regroup(3)
         square(0, 0)
         square(0, 1)
         quantise(1)
@@ -375,33 +394,47 @@ def tile_spatialcgnl_pb_e_kernel(tc, y, Wz_words, Wz_scales, gamma, beta, x, out
             do(stats_bank, s, 0)
             do(sigma_passes, s, 0, HALF)
             do(square, s, 0)
-            do(add_partitions, c)
-            final_step(f, 0)
-            do(regroup, r + 3)
-            do(variance, c)
             if c == 0:
+                add_partitions(c)
+            final_step(f, 0)
+            if r == -1:
+                quantise(2)
+                regroup(4)
+            if c == 0:
+                variance(c)
                 reciprocal_std(c)
             do(stats_bank, s, 1)
             do(sigma_passes, s, HALF, TILES)
             do(square, s, 1)
             if c != 0:
-                do(reciprocal_std, c)
+                do(add_partitions, c)
             final_step(f, 1)
-            do(quantise, r + 3)
+            if c != 0:
+                do(variance, c)
+            if r == -1:
+                quantise(3)
+            if r == 0:
+                regroup(5)
             do(sigma_sum, s)
             do(stats_bank, s, 2)
             do(square, s, 2)
+            if c != 0:
+                do(reciprocal_std, c)
+            if c != 0:
+                final_step(f, 2)
             do(make_neg_mean_over_std, c)
             do(make_gain, c)
             do(make_shift, c)
             do(shift_x_by, c, "V")
             do(shift_x_by, c, "G")
             if c == 0:
-                shift_x_by(c, "S")
-            final_step(f, 2)
+                final_step(f, 2)
+            if r == 0:
+                quantise(4)
+            if r == 1:
+                quantise(5)
             do(stats_bank, s, 3)
             do(square, s, 3)
             do(join_squares, s)
-            if c != 0:
-                do(shift_x_by, c, "S")
+            do(shift_x_by, c, "S")
             final_step(f, 3)

@@ -374,9 +374,9 @@ def tile_spatialcgnl_pb_e_kernel(tc, y, Wz_words, Wz_scales, gamma, beta, x, out
         quantise(0)
         stats_bank(0, 0)
         stats_bank(0, 1)
+        sigma_passes(0, 0, HALF)
         final_bank(0, 2)
         final_bank(0, 3)
-        sigma_passes(0, 0, HALF)
         regroup(1)
         regroup(2)
         regroup(3)
@@ -394,41 +394,33 @@ def tile_spatialcgnl_pb_e_kernel(tc, y, Wz_words, Wz_scales, gamma, beta, x, out
             do(stats_bank, s, 0)
             do(sigma_passes, s, 0, HALF)
             do(square, s, 0)
-            if c == 0:
-                add_partitions(c)
             final_step(f, 0)
             if r == -1:
                 quantise(2)
                 regroup(4)
-            if c == 0:
-                variance(c)
-                reciprocal_std(c)
             do(stats_bank, s, 1)
             do(sigma_passes, s, HALF, TILES)
             do(square, s, 1)
-            if c != 0:
-                do(add_partitions, c)
+            do(add_partitions, c)
             final_step(f, 1)
-            if c != 0:
-                do(variance, c)
-            if r == -1:
-                quantise(3)
+            do(variance, c)
             if r == 0:
                 regroup(5)
             do(sigma_sum, s)
+            if c == 0:
+                reciprocal_std(c)
             do(stats_bank, s, 2)
             do(square, s, 2)
             if c != 0:
                 do(reciprocal_std, c)
-            if c != 0:
-                final_step(f, 2)
+            final_step(f, 2)
             do(make_neg_mean_over_std, c)
             do(make_gain, c)
             do(make_shift, c)
             do(shift_x_by, c, "V")
             do(shift_x_by, c, "G")
-            if c == 0:
-                final_step(f, 2)
+            if r == -1:
+                quantise(3)
             if r == 0:
                 quantise(4)
             if r == 1:

@@ -335,6 +335,13 @@ def tile_spatialcgnl_pb_e_kernel(tc, y, Wz_words, Wz_scales, gamma, beta, x, out
                 mx_pass(zf[:, t, :], u, k * TILES_PER_BANK + t, True, True)
             final_banks[u, k] = zf
 
+        def store(u, first, count):
+            j, b = slabs[u]
+            nc.sync.dma_start(
+                out=out_rows[b, :, j * TILES + first : j * TILES + first + count, :],
+                in_=result[:, u, first : first + count, :],
+            )
+
         def finish(u, k):
             for t in range(TILES_PER_BANK):
                 m = k * TILES_PER_BANK + t
@@ -346,13 +353,8 @@ def tile_spatialcgnl_pb_e_kernel(tc, y, Wz_words, Wz_scales, gamma, beta, x, out
                     op0=ALU.mult,
                     op1=ALU.add,
                 )
-
-        def store(u, first, count):
-            j, b = slabs[u]
-            nc.sync.dma_start(
-                out=out_rows[b, :, j * TILES + first : j * TILES + first + count, :],
-                in_=result[:, u, first : first + count, :],
-            )
+                if u == n_slabs - 1 and k == BANKS - 1:
+                    store(u, m, 1)
 
         def do(step, u, *more):
             if 0 <= u < n_slabs:
@@ -365,7 +367,8 @@ def tile_spatialcgnl_pb_e_kernel(tc, y, Wz_words, Wz_scales, gamma, beta, x, out
             final_bank(u, k)
             finish(u, k)
             if u == n_slabs - 1:
-                store(u, k * TILES_PER_BANK, TILES_PER_BANK)
+                if k != BANKS - 1:
+                    store(u, k * TILES_PER_BANK, TILES_PER_BANK)
             elif i % 2 == 1:
                 store(u, (k - 1) * TILES_PER_BANK, HALF)
 

from contextlib import ExitStack

import concourse.mybir as mybir
from concourse.masks import make_identity

F32 = mybir.dt.float32
BF16 = mybir.dt.bfloat16
I32 = mybir.dt.int32
U32 = mybir.dt.uint32
U8 = mybir.dt.uint8
FP8X4 = mybir.dt.float8_e4m3fn_x4
ALU = mybir.AluOpType
ACT = mybir.ActivationFunctionType

IMAGES = 3
GROUPS = 2
K = 512
CHANNELS = 1024
POSITIONS = 256
EPS = 1e-5

P = 128
PACK = 4
TILES = CHANNELS // P
TILES_PER_BANK = 512 // POSITIONS
BANKS = TILES // TILES_PER_BANK
BANK_COLS = TILES_PER_BANK * POSITIONS
QUADRANTS = 4
BLOCKS_PER_QUADRANT = 4
COUNT = CHANNELS * POSITIONS
LEAD = 2
HALF = TILES // 2
BN_STATS_DIM = 6
OWNERS = ("GGVGVVGG", "VGGGVGGG", "VGGGVGGG", "VGGGVGGG", "SGSGSGSG", "SGSGSGSS")
WARM_MATMULS = 5
REGROUPED_BY_GPSIMD = (2, 3)
VECTOR_BANKS = (2, 3)

FLOPS = 2 * IMAGES * GROUPS * CHANNELS * K * POSITIONS


def tile_spatialcgnl_pb_e_kernel(tc, y, Wz_words, Wz_scales, gamma, beta, x, out):
    nc = tc.nc
    slabs = [(j, b) for j in range(GROUPS) for b in range(IMAGES)]
    n_slabs = len(slabs)

    y_rows = y.rearrange("b j (p t) n -> b j p t n", t=PACK)
    x_rows = x.rearrange("b (r p) h w -> b p r (h w)", p=P)
    out_rows = out.rearrange("b (r p) h w -> b p r (h w)", p=P)
    words_i32 = Wz_words.rearrange("j p n t -> j p (n t)").bitcast(I32)
    scales_i32 = Wz_scales.bitcast(I32)
    gamma_rows = gamma.rearrange("(r p) -> r p", p=P)
    beta_rows = beta.rearrange("(r p) -> r p", p=P)
    affine_rows = GROUPS * TILES

    with ExitStack() as ctx:
        ctx.enter_context(tc.manual_schedule())
        keep = ctx.enter_context(tc.tile_pool(name="keep", bufs=1))
        scratch = ctx.enter_context(tc.tile_pool(name="scratch", bufs=3))
        psum_stats = ctx.enter_context(tc.psum_pool(name="psum_stats", bufs=3))
        psum_final = ctx.enter_context(tc.psum_pool(name="psum_final", bufs=3))
        psum_sigma = ctx.enter_context(tc.psum_pool(name="psum_sigma", bufs=1))
        psum_small = ctx.enter_context(tc.psum_pool(name="psum_small", bufs=1))

        w_words = keep.tile([P, GROUPS, CHANNELS], U32, align_bytes=64)
        w_planes = keep.tile([P, CHANNELS], U8, align_bytes=64)
        y_raw = keep.tile([P, n_slabs, PACK, POSITIONS], BF16)
        y_grouped = keep.tile([P, n_slabs, POSITIONS, PACK], BF16, align_bytes=64)
        y_words = keep.tile([P, n_slabs, POSITIONS], U32, align_bytes=64)
        y_planes = keep.tile([P, n_slabs, POSITIONS], U8, align_bytes=64)
        x_sb = keep.tile([P, n_slabs, TILES, POSITIONS], BF16)
        x_shifted = keep.tile([P, n_slabs, TILES, POSITIONS], F32)
        result = keep.tile([P, n_slabs, TILES, POSITIONS], F32)
        stat = keep.tile([P, n_slabs, 8], F32)
        neg_var = keep.tile([P, n_slabs], F32)
        rstd = keep.tile([P, n_slabs], F32)
        neg_mean_over_std = keep.tile([P, n_slabs], F32)
        gain = keep.tile([P, n_slabs, TILES], F32)
        shift = keep.tile([P, n_slabs, TILES], F32)

        nc.vector.memset(w_planes[:].bitcast(I32), 0)
        affine_in = keep.tile([P, P], BF16)
        nc.vector.memset(affine_in[:], 0.0)
        nc.scalar.dma_start(out=affine_in[0:affine_rows, :], in_=gamma_rows)
        nc.scalar.dma_start(out=affine_in[affine_rows : 2 * affine_rows, :], in_=beta_rows)
        eps = keep.tile([P, 1], F32)
        nc.vector.memset(eps[:], EPS)
        warm = keep.tile([P, 1], F32)
        nc.scalar.activation(out=warm[:], in_=eps[:], func=ACT.Abs_reciprocal_sqrt)
        share = keep.tile([P, P], F32)
        nc.vector.memset(share[:], -1.0 / COUNT)
        share_of_means = keep.tile([P, P], F32)
        nc.vector.memset(share_of_means[:], -float(len(VECTOR_BANKS) * BANK_COLS) / COUNT)
        moments = keep.tile([P, len(VECTOR_BANKS), BN_STATS_DIM], F32)
        means = keep.tile([P, 2], F32)
        identity = keep.tile([P, P], BF16)
        make_identity(nc, identity[:])
        warm_rhs = keep.tile([P, BANK_COLS], BF16)
        nc.vector.memset(warm_rhs[:], 0.0)
        warm_ps = psum_sigma.tile([P, BANK_COLS], F32, tag="sigma")
        for i in range(WARM_MATMULS):
            nc.tensor.matmul(out=warm_ps[:], lhsT=identity[:], rhs=warm_rhs[:], start=True, stop=True)

        def load_weight(j, half):
            cols = slice(half * HALF * P, (half + 1) * HALF * P)
            nc.sync.dma_start(out=w_words[:, j, cols].bitcast(I32), in_=words_i32[j, :, cols])

        def load_y(u):
            j, b = slabs[u]
            nc.sync.dma_start(out=y_raw[:, u], in_=y_rows[b, j])

        def load_x(u):
            j, b = slabs[u]
            for half in range(2):
                first = half * HALF
                nc.sync.dma_start(
                    out=x_sb[:, u, first : first + HALF, :],
                    in_=x_rows[b, :, j * TILES + first : j * TILES + first + HALF, :],
                )

        def load_planes():
            live = GROUPS * BLOCKS_PER_QUADRANT
            for quadrant in range(QUADRANTS):
                blocks = slice(quadrant * BLOCKS_PER_QUADRANT, (quadrant + 1) * BLOCKS_PER_QUADRANT)
                nc.sync.dma_start(
                    out=w_planes[:].bitcast(I32)[32 * quadrant : 32 * quadrant + live, :],
                    in_=scales_i32[:, blocks, :],
                )

        load_y(0)
        load_planes()
        load_weight(0, 0)
        load_y(1)
        load_weight(0, 1)
        load_y(2)
        load_y(3)
        load_y(4)
        load_x(0)
        load_y(5)
        load_x(1)
        load_weight(1, 0)
        load_weight(1, 1)
        for u in range(2, n_slabs):
            load_x(u)

        affine_cols = keep.tile([P, 2 * affine_rows], F32)

        small_bank = psum_small.tile([P, BANK_COLS], F32)
        affine_ps = small_bank[:, BANK_COLS // 2 : BANK_COLS // 2 + P // 2].bitcast(BF16)

        def spread_affine():
            nc.tensor.transpose(affine_ps, affine_in[:], identity[:])
            nc.vector.tensor_copy(out=affine_cols[:], in_=affine_ps[:, 0 : 2 * affine_rows])

        stats_banks, final_banks, sigma, totals = {}, {}, {}, {}

        def regroup(u):
            if u in REGROUPED_BY_GPSIMD:
                nc.gpsimd.tensor_scalar(
                    out=y_grouped[:, u],
                    in0=y_raw[:, u].rearrange("p t n -> p n t"),
                    scalar1=1.0,
                    scalar2=0.0,
                    op0=ALU.mult,
                    op1=ALU.add,
                )
            else:
                nc.vector.tensor_copy(
                    out=y_grouped[:, u].rearrange("p (c i) t -> p c t i", i=4),
                    in_=y_raw[:, u].rearrange("p t (c i) -> p c t i", i=4),
                )

        def quantise(u):
            nc.vector.quantize_mx(
                out=y_words[:, u, :].bitcast(FP8X4),
                scales=y_planes[:, u, :],
                in_=y_grouped[:, u].rearrange("p n t -> p (n t)"),
            )

        def mx_pass(dest, u, m, start, stop):
            j = slabs[u][0]
            cols = slice(m * P, (m + 1) * P)
            nc.tensor.matmul_mx(
                out=dest,
                lhsT=w_words[:, j, cols].bitcast(FP8X4),
                lhsT_scale=w_planes[BLOCKS_PER_QUADRANT * j : P, cols],
                rhs=y_words[:, u, :].bitcast(FP8X4),
                rhs_scale=y_planes[:, u, :],
                start=start,
                stop=stop,
            )

        def stats_bank(u, k):
            zs = psum_stats.tile([P, TILES_PER_BANK, POSITIONS], F32)
            for t in range(TILES_PER_BANK):
                mx_pass(zs[:, t, :], u, k * TILES_PER_BANK + t, True, True)
            stats_banks[u, k] = zs

        def scalar_tiles(u):
            return HALF if u == 0 else TILES

        def sigma_passes(u, first, last):
            if first == 0:
                sg = psum_sigma.tile([P, BANK_COLS], F32, tag="sigma")
                sigma[u] = sg
            for m in range(first, last):
                mx_pass(sigma[u][:, 0:POSITIONS], u, m, m == 0, m == scalar_tiles(u) - 1)

        def moments_of(u, k):
            nc.vector.bn_stats(
                out=moments[:, VECTOR_BANKS.index(k), :], in_=final_banks[u, k][:].rearrange("p t n -> p (t n)")
            )

        def aggregate():
            nc.vector.bn_aggr(out=means[:], in_=moments[:].rearrange("p k s -> p (k s)"))

        def second_moment():
            nc.vector.scalar_tensor_tensor(
                out=means[:, 1:2],
                in0=means[:, 0:1],
                scalar=means[:, 0:1],
                in1=means[:, 1:2],
                op0=ALU.mult,
                op1=ALU.add,
            )

        def square(u, k):
            squares = scratch.tile([P, BANK_COLS], BF16)
            nc.scalar.activation(
                out=squares[:],
                in_=stats_banks[u, k][:].rearrange("p t n -> p (t n)"),
                func=ACT.Square,
                accum_out=stat[:, u, k : k + 1],
            )

        def sigma_sum(u):
            copied = scratch.tile([P, POSITIONS], BF16)
            nc.scalar.activation(
                out=copied[:], in_=sigma[u][:, 0:POSITIONS], func=ACT.Identity, accum_out=stat[:, u, 4:5]
            )

        def join_squares(u):
            four = scratch.tile([P, BANKS], F32)
            n = scalar_tiles(u) // TILES_PER_BANK
            nc.scalar.activation(out=four[:, 0:n], in_=stat[:, u, 0:n], func=ACT.Identity, accum_out=stat[:, u, 5:6])

        def add_partitions(u):
            totals[u] = small_bank[:, 2 * u : 2 * u + 2]
            if u == 0:
                nc.tensor.matmul(out=totals[u], lhsT=share_of_means[:], rhs=means[:], start=True, stop=False)
            nc.tensor.matmul(out=totals[u], lhsT=share[:], rhs=stat[:, u, 4:6], start=(u != 0), stop=True)

        def variance(u):
            nc.vector.tensor_scalar(
                out=neg_var[:, u : u + 1],
                in0=totals[u][:, 0:1],
                scalar1=totals[u][:, 0:1],
                scalar2=totals[u][:, 1:2],
                op0=ALU.mult,
                op1=ALU.add,
            )

        def reciprocal_std(u):
            nc.scalar.activation(
                out=rstd[:, u : u + 1],
                in_=neg_var[:, u : u + 1],
                func=ACT.Abs_reciprocal_sqrt,
                scale=-1.0,
                bias=eps[:],
            )

        def make_gain(u):
            j = slabs[u][0]
            nc.vector.tensor_scalar_mul(
                out=gain[:, u, :], in0=affine_ps[:, j * TILES : (j + 1) * TILES], scalar1=rstd[:, u : u + 1]
            )

        def make_neg_mean_over_std(u):
            nc.vector.tensor_scalar_mul(
                out=neg_mean_over_std[:, u : u + 1], in0=totals[u][:, 0:1], scalar1=rstd[:, u : u + 1]
            )

        def make_shift(u):
            j = slabs[u][0]
            nc.vector.scalar_tensor_tensor(
                out=shift[:, u, :],
                in0=affine_ps[:, j * TILES : (j + 1) * TILES],
                scalar=neg_mean_over_std[:, u : u + 1],
                in1=affine_cols[:, affine_rows + j * TILES : affine_rows + (j + 1) * TILES],
                op0=ALU.mult,
                op1=ALU.add,
            )

        def shift_x(u, m, owner):
            if owner == "V":
                nc.vector.tensor_scalar(
                    out=x_shifted[:, u, m, :],
                    in0=x_sb[:, u, m, :],
                    scalar1=shift[:, u, m : m + 1],
                    scalar2=None,
                    op0=ALU.add,
                )
            elif owner == "S":
                nc.scalar.activation(
                    out=x_shifted[:, u, m, :],
                    in_=x_sb[:, u, m, :],
                    func=ACT.Identity,
                    bias=shift[:, u, m : m + 1],
                )
            else:
                nc.gpsimd.tensor_scalar(
                    out=x_shifted[:, u, m, :],
                    in0=x_sb[:, u, m, :],
                    scalar1=1.0,
                    scalar2=shift[:, u, m : m + 1],
                    op0=ALU.mult,
                    op1=ALU.add,
                )

        def final_order(u):
            return (2, 3, 0, 1) if u == 0 else (0, 1, 2, 3)

        def shift_x_by(u, owner):
            owners = OWNERS[u]
            for k in final_order(u):
                for m in range(k * TILES_PER_BANK, (k + 1) * TILES_PER_BANK):
                    if owners[m] == owner:
                        shift_x(u, m, owner)

        def final_bank(u, k):
            if (u, k) in final_banks:
                return
            zf = psum_final.tile([P, TILES_PER_BANK, POSITIONS], F32)
            for t in range(TILES_PER_BANK):
                mx_pass(zf[:, t, :], u, k * TILES_PER_BANK + t, True, True)
            final_banks[u, k] = zf

        def store(u, first, count):
            j, b = slabs[u]
            nc.sync.dma_start(
                out=out_rows[b, :, j * TILES + first : j * TILES + first + count, :],
                in_=result[:, u, first : first + count, :],
            )

        def finish(u, k):
            for t in range(TILES_PER_BANK):
                m = k * TILES_PER_BANK + t
                nc.vector.scalar_tensor_tensor(
                    out=result[:, u, m, :],
                    in0=final_banks[u, k][:, t, :],
                    scalar=gain[:, u, m : m + 1],
                    in1=x_shifted[:, u, m, :],
                    op0=ALU.mult,
                    op1=ALU.add,
                )
                if u == n_slabs - 1 and k == BANKS - 1:
                    store(u, m, 1)

        def do(step, u, *more):
            if 0 <= u < n_slabs:
                step(u, *more)

        def final_step(u, i):
            if not 0 <= u < n_slabs:
                return
            k = final_order(u)[i]
            final_bank(u, k)
            finish(u, k)
            if u == n_slabs - 1:
                if k != BANKS - 1:
                    store(u, k * TILES_PER_BANK, TILES_PER_BANK)
            elif i % 2 == 1:
                store(u, (k - 1) * TILES_PER_BANK, HALF)

        regroup(0)
        spread_affine()
        quantise(0)
        stats_bank(0, 0)
        stats_bank(0, 1)
        sigma_passes(0, 0, HALF)
        final_bank(0, 2)
        final_bank(0, 3)
        regroup(1)
        regroup(2)
        regroup(3)
        square(0, 0)
        square(0, 1)
        quantise(1)
        moments_of(0, 2)
        moments_of(0, 3)
        aggregate()
        second_moment()
        sigma_sum(0)
        join_squares(0)
        for r in range(-1, n_slabs):
            s, c, f = r + LEAD, r + LEAD - 1, r
            do(stats_bank, s, 0)
            do(sigma_passes, s, 0, HALF)
            do(square, s, 0)
            final_step(f, 0)
            if r == -1:
                quantise(2)
                regroup(4)
            do(stats_bank, s, 1)
            do(sigma_passes, s, HALF, TILES)
            do(square, s, 1)
            do(add_partitions, c)
            final_step(f, 1)
            do(variance, c)
            if r == 0:
                regroup(5)
            do(sigma_sum, s)
            if c == 0:
                reciprocal_std(c)
            do(stats_bank, s, 2)
            do(square, s, 2)
            if c != 0:
                do(reciprocal_std, c)
            final_step(f, 2)
            do(make_neg_mean_over_std, c)
            do(make_gain, c)
            do(make_shift, c)
            do(shift_x_by, c, "V")
            do(shift_x_by, c, "G")
            if r == -1:
                quantise(3)
            if r == 0:
                quantise(4)
            if r == 1:
                quantise(5)
            do(stats_bank, s, 3)
            do(square, s, 3)
            do(join_squares, s)
            do(shift_x_by, c, "S")
            final_step(f, 3)
